import numpy as np
import ml_dtypes


def mxq(x, axis, fmt="e4m3"):
    dtype, down = {"e4m3": (ml_dtypes.float8_e4m3fn, 7), "e5m2": (ml_dtypes.float8_e5m2, 14)}[fmt]
    v = np.moveaxis(np.asarray(x, np.float32).astype(ml_dtypes.bfloat16).astype(np.float64), axis, -1)
    blocks = v.reshape(v.shape[:-1] + (-1, 32))
    amax = np.abs(blocks).max(-1, keepdims=True)
    byte = np.maximum(np.where(amax > 0, np.frexp(amax)[1] - 1 + 127, 0) - down, 1)
    scale = np.exp2(byte - 127.0)
    codes = (blocks / scale).astype(np.float32).astype(dtype).astype(np.float64)
    return np.moveaxis((codes * scale).reshape(v.shape), -1, axis)


WIDE = False


def mx_kscale(k):
    if not WIDE:
        return np.ones(k)
    levels = np.array([10, -10, 5, -5, 0])
    if k % 512:
        return np.exp2(np.random.permutation(np.resize(levels, k // 32))).repeat(32)
    a = np.empty((k // 512, 16))
    for p in range(k // 512):
        a[p, :8] = np.random.permutation(np.resize(levels, 8))
        for g in range(8):
            far = levels[np.abs(levels - a[p, g]) >= 10]
            a[p, g + 8] = far[np.random.randint(len(far))]
    return np.exp2(a.ravel()).repeat(32)


BF16 = ml_dtypes.bfloat16


def bf(x):
    return np.asarray(x, np.float32).astype(BF16)


def f64(x):
    return np.asarray(x).astype(np.float64)


B, J, C, K, H = 8, 128, 512, 4, 256
KJ = K * J
EPS = 1e-5


def layernorm(v, g, b):
    m = v.mean(-1, keepdims=True)
    var = v.var(-1, keepdims=True)
    return (v - m) / np.sqrt(var + EPS) * g + b


def gcn(xin, adj, spatial_adj, conv_w, conv_b, s_ctx):
    h = (mxq(xin, 2, "e4m3") @ mxq(conv_w, 1, "e4m3").T) + conv_b
    h = h.reshape(B, J, K, C).transpose(0, 2, 1, 3).reshape(B, KJ, C)
    sadj = np.broadcast_to(spatial_adj[None], (B, K - 1, J, J))
    adj4 = np.concatenate([adj * s_ctx, sadj], axis=1).reshape(B, KJ, J)
    return mxq(adj4, 1, "e4m3").transpose(0, 2, 1) @ mxq(h, 1, "e4m3")


def draw0():
    s = mx_kscale(C)
    t = np.sort(mx_kscale(KJ))[np.arange(K) * (KJ - 1) // (K - 1)]
    tw = np.repeat(t, C)
    a = 2.0 / np.sqrt(KJ)
    return {"g1": bf(np.random.standard_normal((B, J, C)) * 0.9 * s),
            "res1": bf(np.random.standard_normal((B, J, C))),
            "adj": bf(np.random.random((B, 1, J, J)) * a / t[0]),
            "spatial_adj": bf(np.random.random((K - 1, J, J)) * a / t[1:, None, None]),
            "conv2_w": bf(np.random.standard_normal((K * C, C)) / np.sqrt(C) / s[None, :] * tw[:, None]),
            "conv2_b": bf(np.random.standard_normal(K * C) * 0.05 * tw),
            "s2": bf(1.5 + 0.1 * np.random.standard_normal(1)),
            "norm2_g": bf(1.0 + 0.1 * np.random.standard_normal(C)),
            "norm2_b": bf(0.1 * np.random.standard_normal(C))}


def core(g1, res1, adj, spatial_adj, conv2_w, conv2_b, s2, norm2_g, norm2_b):
    g2 = gcn(f64(g1), f64(adj), f64(spatial_adj), f64(conv2_w), f64(conv2_b), f64(s2))
    x2 = f64(res1) + g2
    xn = layernorm(x2, f64(norm2_g), f64(norm2_b))
    return x2, xn


def e4m3fn_bytes(y):
    return np.clip(np.asarray(y, np.float64), -448.0, 448.0).astype(np.float32).astype(ml_dtypes.float8_e4m3fn).view(np.uint8)


def e4m3fn_values(b):
    return np.asarray(b, np.uint8).view(ml_dtypes.float8_e4m3fn).astype(np.float64)


def setup_inputs():
    d = draw0()
    x0 = np.asarray(d['g1']).astype(np.float64)
    s = (np.max(np.abs(x0), axis=(0, 1), keepdims=True) / 448.0).astype(np.float32)
    out = {}
    for k, v in d.items():
        if k == 'g1':
            out['g1_bytes'] = e4m3fn_bytes(x0 / s.astype(np.float64))
            out['g1_scale'] = s
        else:
            out[k] = v
    return out


def reference(g1_bytes, g1_scale, res1, adj, spatial_adj, conv2_w, conv2_b, s2, norm2_g, norm2_b):
    return core(e4m3fn_values(g1_bytes) * g1_scale.astype(np.float64), res1, adj, spatial_adj, conv2_w, conv2_b, s2, norm2_g, norm2_b)

@@ -1,0 +1,496 @@
+from contextlib import ExitStack
+
+import concourse.mybir as mybir
+from concourse.masks import make_identity
+
+F32 = mybir.dt.float32
+BF16 = mybir.dt.bfloat16
+U32 = mybir.dt.uint32
+U8 = mybir.dt.uint8
+FP8 = mybir.dt.float8_e4m3fn
+FP8X4 = mybir.dt.float8_e4m3fn_x4
+ALU = mybir.AluOpType
+ACT = mybir.ActivationFunctionType
+
+B, J, C, K = 8, 128, 512, 4
+P = 128
+PAIRS = B // 2
+GROUPS = ((0, 4), (4, 4),)
+NCC = C // P
+EPS = 1e-5
+
+FLOPS = 2 * B * J * C * K * C + 2 * B * K * J * J * C
+
+TP_BANKS = 3
+
+
+def tile_block_attention_guide_pb_kernel(
+    tc, g1_bytes, g1_scale, res1, adj, spatial_adj, conv2_w, conv2_b, s2, norm2_g, norm2_b, out_0, out_1
+):
+    nc = tc.nc
+    with ExitStack() as ctx:
+        keep = ctx.enter_context(tc.tile_pool(name="keep", bufs=1))
+        work = ctx.enter_context(tc.tile_pool(name="work", bufs=3))
+        psum = ctx.enter_context(tc.psum_pool(name="psum", bufs=1))
+        ctx.enter_context(tc.manual_schedule())
+
+        def keep_tile(name, shape, dt):
+            return keep.tile(shape, dt, name=name, align_bytes=64)
+
+        gb = [keep_tile("gb%d" % q, [P, 2, C], U8) for q in range(PAIRS)]
+        gw = [keep_tile("gw%d" % q, [P, 2, C], BF16) for q in range(PAIRS)]
+        gs = [keep_tile("gs%d" % q, [P, 2 * J, 4], BF16) for q in range(PAIRS)]
+        gc = [keep_tile("gc%d" % g, [P, n * J], U32) for g, (b0, n) in enumerate(GROUPS)]
+        gsc = [keep_tile("gsc%d" % g, [P, n * J], U8) for g, (b0, n) in enumerate(GROUPS)]
+        wr = [keep_tile("wr%d" % j, [P, 2, C], BF16) for j in range(8)]
+        wi = [keep_tile("wi%d" % j, [P, 2 * P, 4], BF16) for j in range(8)]
+        wc = [keep_tile("wc%d" % j, [P, 2 * P], U32) for j in range(8)]
+        wsc = [keep_tile("wsc%d" % j, [P, 2 * P], U8) for j in range(8)]
+        hh = [[keep_tile("hh%d_%d" % (g, cc), [P, 2 * n, K, J // 2], BF16) for cc in range(NCC)] for g, (b0, n) in enumerate(GROUPS)]
+        hq = [[keep_tile("hq%d_%d" % (p, f), [P, 2, C // 2, 4], BF16) for f in range(2)] for p in range(PAIRS)]
+        hc = [[keep_tile("hc%d_%d" % (p, f), [P, C], U32) for f in range(2)] for p in range(PAIRS)]
+        hsc = [[keep_tile("hsc%d_%d" % (p, f), [P, C], U8) for f in range(2)] for p in range(PAIRS)]
+        a_raw = keep_tile("a_raw", [P, B, 4, J], BF16)
+        a_bf = [keep_tile("a_bf%d" % p, [P, 2, J, 4], BF16) for p in range(PAIRS)]
+        ac = [keep_tile("ac%d" % p, [P, 2 * J], U32) for p in range(PAIRS)]
+        asc = [keep_tile("asc%d" % p, [P, 2 * J], U8) for p in range(PAIRS)]
+        res = [keep_tile("res%d" % p, [P, 2, C], BF16) for p in range(PAIRS)]
+        ident = keep_tile("ident", [P, P], F32)
+        perm = keep_tile("perm", [P, P], F32)
+        ident_b = keep_tile("ident_b", [P, P], BF16)
+        brow = keep_tile("brow", [P, P], BF16)
+        bias = keep_tile("bias", [P, K * NCC], F32)
+        gsv = keep_tile("gsv", [P, 4], F32)
+        s2b = keep_tile("s2b", [32, 1], BF16)
+        s2v = keep_tile("s2v", [P, 1], F32)
+        gain = keep_tile("gain", [P, C], BF16)
+        shift = keep_tile("shift", [P, C], BF16)
+        sums = keep_tile("sums", [P, B], F32)
+        nmean = keep_tile("nmean", [P, B], F32)
+        ssq = keep_tile("ssq", [P, B], F32)
+        vare = keep_tile("vare", [P, B], F32)
+        rstd = keep_tile("rstd", [P, B], F32)
+        mhalf = keep_tile("mhalf", [P, 1], F32)
+        warm = keep_tile("warm", [P, 1], F32)
+        zeros = keep_tile("zeros", [P, 512], BF16)
+
+        def tp_tile(dt=F32, n=512):
+            return psum.tile([P, n], dt, name="tp", bufs=TP_BANKS)
+
+        def mm_tile():
+            return psum.tile([P, 512], F32, name="mm", bufs=8 - TP_BANKS)
+
+        g_src = g1_bytes.rearrange("b j c -> j b c")
+        w_src = conv2_w.rearrange("(k cc m) c -> cc m k c", k=K, cc=NCC)
+        r_src = res1.rearrange("b j c -> j b c")
+
+        def load_g(q):
+            nc.sync.dma_start(out=gb[q][:], in_=g_src[:, 2 * q : 2 * q + 2, :])
+
+        def load_w(j):
+            nc.sync.dma_start(out=wr[j][:], in_=w_src[j // 2][:, 2 * (j % 2) : 2 * (j % 2) + 2, :])
+
+        def load_r(p):
+            nc.sync.dma_start(out=res[p][:], in_=r_src[:, 2 * p : 2 * p + 2, :])
+
+        nc.vector.memset(zeros[:].bitcast(U32), 0)
+        nc.vector.memset(warm[:], 0.0)
+        load_g(0)
+        load_w(0)
+        load_g(1)
+        nc.scalar.dma_start(out=gsv[:], in_=g1_scale.rearrange("a b (p t) -> p (a b t)", t=4))
+        nc.scalar.activation(out=warm[:], in_=warm[:], func=ACT.Square)
+        make_identity(nc, ident[:])
+        nc.gpsimd.memset(brow[:], 0.0)
+        nc.scalar.dma_start(out=brow[0 : K * NCC, :], in_=conv2_b.rearrange("(r m) -> r m", m=P))
+        nc.scalar.dma_start(out=s2b[:], in_=s2.partition_broadcast(32))
+        nc.gpsimd.memset(s2v[:], 1.0)
+        nc.gpsimd.memset(mhalf[:], -0.5)
+        for j in range(1, 8):
+            load_w(j)
+        load_g(2)
+        load_g(3)
+        nc.sync.dma_start(out=a_raw[0:32, :, :, :], in_=adj.rearrange("b o (q t) w -> q b (o t w)", t=4))
+        nc.sync.dma_start(
+            out=a_raw[32:P, :, :, :].rearrange("p b t w -> p b (t w)"),
+            in_=spatial_adj.rearrange("k (q t) w -> (k q) (t w)", t=4).unsqueeze(1).to_broadcast([96, B, 512]),
+        )
+        load_r(0)
+        nc.sync.dma_start(out=gain[:], in_=norm2_g.partition_broadcast(P))
+        nc.sync.dma_start(out=shift[:], in_=norm2_b.partition_broadcast(P))
+        for p in range(1, PAIRS):
+            load_r(p)
+
+        nc.vector.tensor_copy(
+            out=perm[:].rearrange("p (u q e) -> p u q e", u=2, e=2),
+            in_=ident[:].rearrange("p (q u e) -> p u q e", u=2, e=2),
+        )
+        nc.vector.tensor_copy(out=ident_b[:], in_=ident[:])
+
+        g_banks, w_banks, h_banks, t_banks, o_banks, x2s, ys = {}, {}, {}, {}, {}, {}, {}
+
+        b_bank = {}
+
+        def either(on_vector):
+            return nc.vector.tensor_copy if on_vector else nc.scalar.copy
+
+        def warm_up(n):
+            bank = mm_tile()
+            for r in range(n):
+                nc.tensor.matmul(out=bank[:], lhsT=zeros[:, 0:P], rhs=zeros[:], start=True, stop=True)
+
+        def bias_transpose():
+            b_bank[0] = tp_tile(BF16, P)
+            nc.tensor.transpose(b_bank[0][:], brow[:], ident_b[:])
+
+        def bias_copy(on_vector):
+            either(on_vector)(out=bias[:], in_=b_bank[0][:, 0 : K * NCC])
+
+        def g_widen(q, on_vector):
+            either(on_vector)(out=gw[q][:], in_=gb[q][:].bitcast(FP8))
+
+        def g_transpose(q):
+            bank = tp_tile()
+            g_banks[q] = bank
+            for bb in range(2):
+                words = gw[q][:, bb, :].bitcast(F32)
+                for u in range(2):
+                    o = 256 * u + 128 * bb
+                    nc.tensor.transpose(bank[:, o : o + 128], words[:, u::2], perm[:])
+
+        def g_scale(q):
+            nc.vector.tensor_tensor(
+                out=gs[q][:].rearrange("p r (u e) -> p r u e", u=2),
+                in0=g_banks[q][:].bitcast(BF16).rearrange("p (u r e) -> p r u e", u=2, e=2),
+                in1=gsv[:].rearrange("p (u e) -> p u e", u=2).unsqueeze(1).to_broadcast([P, 256, 2, 2]),
+                op=ALU.mult,
+            )
+
+        group_of = [g for g, (b0, n) in enumerate(GROUPS) for q in range(n // 2)]
+
+        def g_quant(q):
+            g = group_of[q]
+            o = 2 * J * (q - GROUPS[g][0] // 2)
+            cols = slice(o, o + 2 * J)
+            nc.vector.quantize_mx(out=gc[g][:, cols].bitcast(FP8X4), scales=gsc[g][:, cols], in_=gs[q][:].rearrange("p r t -> p (r t)"))
+
+        def w_transpose(j):
+            bank = tp_tile()
+            w_banks[j] = bank
+            for kk in range(2):
+                words = wr[j][:, kk, :].bitcast(F32)
+                for u in range(2):
+                    o = 256 * u + 128 * kk
+                    nc.tensor.transpose(bank[:, o : o + 128], words[:, u::2], ident[:])
+
+        def w_copy(j, on_vector):
+            either(on_vector)(
+                out=wi[j][:].rearrange("p m t -> p (m t)").bitcast(F32).rearrange("p (m u) -> p m u", u=2),
+                in_=w_banks[j][:].rearrange("p (u m) -> p m u", u=2),
+            )
+
+        def w_quant(j):
+            nc.vector.quantize_mx(out=wc[j][:].bitcast(FP8X4), scales=wsc[j][:], in_=wi[j][:].rearrange("p m t -> p (m t)"))
+
+        def a_scale(p):
+            nc.gpsimd.tensor_scalar(
+                out=a_bf[p][:], in0=a_raw[:, 2 * p : 2 * p + 2, :, :].rearrange("p b t w -> p b w t"),
+                scalar1=s2v[:, 0:1], scalar2=0.0, op0=ALU.mult, op1=ALU.add,
+            )
+
+        def a_quant(p):
+            nc.vector.quantize_mx(out=ac[p][:].bitcast(FP8X4), scales=asc[p][:], in_=a_bf[p][:].rearrange("p b w t -> p (b w t)"))
+
+        def h_matmul(p, i, times=1):
+            j, cols = i // 2, slice(P * (i % 2), P * (i % 2) + P)
+            bank = mm_tile()
+            h_banks[(p, i)] = bank
+            for r in range(times):
+                nc.tensor.matmul_mx(
+                    out=bank[:, 0 : J * GROUPS[p][1]], lhsT=wc[j][:, cols].bitcast(FP8X4), lhsT_scale=wsc[j][:, cols],
+                    rhs=gc[p][:].bitcast(FP8X4), rhs_scale=gsc[p][:], start=True, stop=True,
+                )
+
+        def h_bias(p, i, on_vector):
+            cc, k = i // K, i % K
+            out = hh[p][cc][:, :, k, :]
+            src = h_banks[(p, i)][:, 0 : J * GROUPS[p][1]].rearrange("p (x v) -> p x v", v=64)
+            col = bias[:, k * NCC + cc : k * NCC + cc + 1]
+            if on_vector:
+                nc.vector.tensor_scalar(out=out, in0=src, scalar1=col, scalar2=None, op0=ALU.add)
+            else:
+                nc.scalar.activation(out=out, in_=src, func=ACT.Identity, bias=col)
+
+        def h_transpose(p, cc):
+            bank = tp_tile()
+            t_banks[(p, cc)] = bank
+            g = group_of[p]
+            for x in range(4):
+                words = hh[g][cc][:, 4 * (p - GROUPS[g][0] // 2) + x, :, :].rearrange("p k v -> p (k v)").bitcast(F32)
+                nc.tensor.transpose(bank[:, 128 * x : 128 * x + 128], words, ident[:])
+
+        def h_copy(p, cc, on_vector):
+            c0 = P * (cc % 2)
+            dst = hq[p][cc // 2][:, :, c0 : c0 + P, :].rearrange("p b c t -> p b (c t)").bitcast(F32)
+            either(on_vector)(
+                out=dst.rearrange("p b (c u) -> p b c u", u=2),
+                in_=t_banks[(p, cc)][:].rearrange("p (b u c) -> p b c u", b=2, u=2),
+            )
+
+        def h_quant(p, f):
+            nc.vector.quantize_mx(
+                out=hc[p][f][:].bitcast(FP8X4), scales=hsc[p][f][:], in_=hq[p][f][:].rearrange("p b c t -> p (b c t)")
+            )
+
+        def o_matmul(b, f):
+            p, cols, half = b // 2, slice(J * (b % 2), J * (b % 2) + J), slice(256 * (b % 2), 256 * (b % 2) + 256)
+            if f == 0:
+                o_banks[b] = mm_tile()
+            nc.tensor.matmul_mx(
+                out=o_banks[b][:, 256 * f : 256 * f + 256], lhsT=ac[p][:, cols].bitcast(FP8X4), lhsT_scale=asc[p][:, cols],
+                rhs=hc[p][f][:, half].bitcast(FP8X4), rhs_scale=hsc[p][f][:, half], start=True, stop=True,
+            )
+
+        def residual(b):
+            x2 = work.tile([P, C], F32, name="x2", bufs=4)
+            x2s[b] = x2
+            nc.vector.scalar_tensor_tensor(
+                out=x2[:], in0=o_banks[b][:], scalar=1.0, in1=res[b // 2][:, b % 2, :],
+                op0=ALU.mult, op1=ALU.add, accum_out=sums[:, b : b + 1],
+            )
+            nc.sync.dma_start(out=out_0[b], in_=x2[:])
+            nc.gpsimd.tensor_scalar(
+                out=nmean[:, b : b + 1], in0=sums[:, b : b + 1], scalar1=-1.0 / C, scalar2=0.0, op0=ALU.mult, op1=ALU.add
+            )
+
+        def variance(b):
+            junk = work.tile([P, C], BF16, name="junk", bufs=2)
+            nc.scalar.activation(
+                out=junk[:], in_=x2s[b][:], func=ACT.Square, bias=nmean[:, b : b + 1], accum_out=ssq[:, b : b + 1]
+            )
+            nc.gpsimd.tensor_scalar(
+                out=vare[:, b : b + 1], in0=ssq[:, b : b + 1], scalar1=1.0 / C, scalar2=EPS, op0=ALU.mult, op1=ALU.add
+            )
+            nc.gpsimd.tensor_tensor(out=rstd[:, b : b + 1], in0=vare[:, b : b + 1], in1=mhalf[:], op=ALU.pow)
+
+        def centre(b):
+            y = work.tile([P, C], F32, name="y", bufs=3)
+            ys[b] = y
+            nc.vector.scalar_tensor_tensor(
+                out=y[:], in0=x2s[b][:], scalar=nmean[:, b : b + 1], in1=gain[:], op0=ALU.add, op1=ALU.mult
+            )
+
+        def normalise(b):
+            xn = work.tile([P, C], F32, name="xn", bufs=3)
+            nc.vector.scalar_tensor_tensor(
+                out=xn[:], in0=ys[b][:], scalar=rstd[:, b : b + 1], in1=shift[:], op0=ALU.mult, op1=ALU.add
+            )
+            nc.sync.dma_start(out=out_1[b], in_=xn[:])
+
+        nc.gpsimd.tensor_copy(out=s2v[0:32, :], in_=s2b[:])
+        warm_up(6)
+        g_widen(0, True)
+        w_transpose(0)
+        g_widen(1, False)
+        warm_up(1)
+        w_copy(0, True)
+        g_transpose(0)
+        w_quant(0)
+        g_transpose(1)
+        g_scale(0)
+        warm_up(1)
+        bias_transpose()
+        g_scale(1)
+        warm_up(1)
+        bias_copy(False)
+        w_transpose(1)
+        g_quant(0)
+        g_quant(1)
+        h_matmul(0, 0)
+        g_widen(2, True)
+        w_copy(1, False)
+        g_widen(3, True)
+        w_transpose(2)
+        h_bias(0, 0, True)
+        w_quant(1)
+        w_transpose(3)
+        w_copy(2, False)
+        a_scale(0)
+        w_quant(2)
+        h_matmul(0, 3)
+        w_copy(3, True)
+        h_matmul(0, 2)
+        w_quant(3)
+        a_scale(1)
+        h_bias(0, 3, True)
+        h_matmul(0, 1)
+        h_bias(0, 2, False)
+        w_transpose(4)
+        a_quant(0)
+        h_bias(0, 1, True)
+        h_matmul(0, 4)
+        a_scale(3)
+        w_copy(4, False)
+        a_quant(1)
+        h_matmul(0, 5)
+        h_transpose(1, 0)
+        h_bias(0, 4, False)
+        w_quant(4)
+        w_transpose(5)
+        a_scale(2)
+        h_copy(1, 0, True)
+        h_bias(0, 5, False)
+        h_matmul(0, 7)
+        w_copy(5, True)
+        h_matmul(0, 6)
+        w_transpose(6)
+        h_bias(0, 7, True)
+        h_bias(0, 6, False)
+        h_matmul(0, 8)
+        w_quant(5)
+        w_copy(6, False)
+        h_transpose(1, 1)
+        a_quant(2)
+        h_bias(0, 8, True)
+        h_transpose(0, 1)
+        h_copy(1, 1, False)
+        h_matmul(0, 10)
+        w_quant(6)
+        h_matmul(0, 9)
+        h_copy(0, 1, False)
+        a_quant(3)
+        w_transpose(7)
+        h_quant(1, 0)
+        h_bias(0, 9, False)
+        g_transpose(2)
+        h_bias(0, 10, True)
+        h_transpose(0, 0)
+        w_copy(7, True)
+        h_matmul(0, 13)
+        h_copy(0, 0, False)
+        h_matmul(0, 12, 2)
+        g_scale(2)
+        h_bias(0, 13, False)
+        g_transpose(3)
+        h_bias(0, 12, False)
+        w_quant(7)
+        h_matmul(0, 11)
+        h_quant(0, 0)
+        h_matmul(0, 14, 2)
+        h_bias(0, 11, False)
+        g_scale(3)
+        h_matmul(0, 15, 2)
+        h_bias(0, 14, False)
+        h_transpose(1, 2)
+        h_bias(0, 15, False)
+        h_transpose(0, 2)
+        g_quant(2)
+        g_quant(3)
+        h_copy(1, 2, False)
+        h_transpose(0, 3)
+        h_matmul(1, 2)
+        h_copy(0, 2, False)
+        h_copy(0, 3, True)
+        h_matmul(1, 7, 2)
+        h_bias(1, 2, False)
+        h_matmul(1, 3)
+        h_quant(0, 1)
+        h_matmul(1, 0)
+        h_bias(1, 3, False)
+        h_matmul(1, 1)
+        h_bias(1, 7, True)
+        o_matmul(0, 0)
+        o_matmul(0, 1)
+        h_bias(1, 0, False)
+        h_transpose(1, 3)
+        residual(0)
+        o_matmul(1, 0)
+        o_matmul(1, 1)
+        h_bias(1, 1, False)
+        h_copy(1, 3, True)
+        h_matmul(1, 5)
+        variance(0)
+        h_matmul(1, 6)
+        residual(1)
+        h_transpose(3, 0)
+        h_bias(1, 5, False)
+        h_transpose(2, 0)
+        centre(0)
+        h_matmul(1, 4, 2)
+        h_bias(1, 6, False)
+        h_copy(2, 0, True)
+        h_matmul(1, 10)
+        variance(1)
+        centre(1)
+        h_matmul(1, 9)
+        h_matmul(1, 14)
+        h_bias(1, 4, False)
+        normalise(0)
+        h_matmul(1, 15)
+        h_bias(1, 9, False)
+        h_matmul(1, 11)
+        normalise(1)
+        h_transpose(2, 1)
+        h_bias(1, 10, False)
+        h_quant(1, 1)
+        h_bias(1, 11, False)
+        h_matmul(1, 8)
+        h_copy(2, 1, True)
+        o_matmul(2, 0)
+        o_matmul(2, 1)
+        h_copy(3, 0, False)
+        h_bias(1, 15, True)
+        h_bias(1, 14, False)
+        h_transpose(3, 1)
+        residual(2)
+        h_bias(1, 8, False)
+        h_matmul(1, 13)
+        h_quant(2, 0)
+        h_matmul(1, 12)
+        h_copy(3, 1, False)
+        h_transpose(3, 2)
+        centre(2)
+        h_bias(1, 12, False)
+        h_transpose(2, 2)
+        h_bias(1, 13, True)
+        o_matmul(3, 0)
+        o_matmul(3, 1)
+        variance(2)
+        h_quant(3, 0)
+        h_transpose(2, 3)
+        h_copy(2, 2, False)
+        residual(3)
+        h_copy(2, 3, False)
+        normalise(2)
+        h_copy(3, 2, False)
+        centre(3)
+        variance(3)
+        h_transpose(3, 3)
+        h_quant(2, 1)
+        h_copy(3, 3, False)
+        o_matmul(4, 0)
+        o_matmul(4, 1)
+        normalise(3)
+        o_matmul(5, 0)
+        o_matmul(5, 1)
+        h_quant(3, 1)
+        residual(5)
+        o_matmul(6, 0)
+        o_matmul(6, 1)
+        residual(4)
+        o_matmul(7, 0)
+        o_matmul(7, 1)
+        variance(5)
+        centre(5)
+        variance(4)
+        centre(4)
+        normalise(5)
+        residual(7)
+        residual(6)
+        variance(7)
+        centre(7)
+        variance(6)
+        centre(6)
+        normalise(7)
+        normalise(6)
+        normalise(4)

@@ -14,14 +14,14 @@ ACT = mybir.ActivationFunctionType
 
 B, J, C, K = 8, 128, 512, 4
 P = 128
+HALF = 4
 PAIRS = B // 2
-GROUPS = ((0, 4), (4, 4),)
 NCC = C // P
 EPS = 1e-5
 
 FLOPS = 2 * B * J * C * K * C + 2 * B * K * J * J * C
 
-TP_BANKS = 3
+TP_BANKS = 4
 
 
 def tile_block_attention_guide_pb_kernel(
@@ -37,16 +37,16 @@ def tile_block_attention_guide_pb_kernel(
         def keep_tile(name, shape, dt):
             return keep.tile(shape, dt, name=name, align_bytes=64)
 
-        gb = [keep_tile("gb%d" % q, [P, 2, C], U8) for q in range(PAIRS)]
-        gw = [keep_tile("gw%d" % q, [P, 2, C], BF16) for q in range(PAIRS)]
-        gs = [keep_tile("gs%d" % q, [P, 2 * J, 4], BF16) for q in range(PAIRS)]
-        gc = [keep_tile("gc%d" % g, [P, n * J], U32) for g, (b0, n) in enumerate(GROUPS)]
-        gsc = [keep_tile("gsc%d" % g, [P, n * J], U8) for g, (b0, n) in enumerate(GROUPS)]
+        gb = [keep_tile("gb%d" % h, [P, 2, 2, C], U8) for h in range(2)]
+        gw = [[keep_tile("gw%d_%d" % (h, j), [P, 2, C], BF16) for j in range(2)] for h in range(2)]
+        gs = [keep_tile("gs%d" % h, [P, HALF * J, 4], BF16) for h in range(2)]
+        gc = [keep_tile("gc%d" % h, [P, HALF * J], U32) for h in range(2)]
+        gsc = [keep_tile("gsc%d" % h, [P, HALF * J], U8) for h in range(2)]
         wr = [keep_tile("wr%d" % j, [P, 2, C], BF16) for j in range(8)]
         wi = [keep_tile("wi%d" % j, [P, 2 * P, 4], BF16) for j in range(8)]
         wc = [keep_tile("wc%d" % j, [P, 2 * P], U32) for j in range(8)]
         wsc = [keep_tile("wsc%d" % j, [P, 2 * P], U8) for j in range(8)]
-        hh = [[keep_tile("hh%d_%d" % (g, cc), [P, 2 * n, K, J // 2], BF16) for cc in range(NCC)] for g, (b0, n) in enumerate(GROUPS)]
+        hh = [[keep_tile("hh%d_%d" % (h, cc), [P, 2 * HALF, K, J // 2], BF16) for cc in range(NCC)] for h in range(2)]
         hq = [[keep_tile("hq%d_%d" % (p, f), [P, 2, C // 2, 4], BF16) for f in range(2)] for p in range(PAIRS)]
         hc = [[keep_tile("hc%d_%d" % (p, f), [P, C], U32) for f in range(2)] for p in range(PAIRS)]
         hsc = [[keep_tile("hsc%d_%d" % (p, f), [P, C], U8) for f in range(2)] for p in range(PAIRS)]
@@ -57,16 +57,14 @@ def tile_block_attention_guide_pb_kernel(
         res = [keep_tile("res%d" % p, [P, 2, C], BF16) for p in range(PAIRS)]
         ident = keep_tile("ident", [P, P], F32)
         perm = keep_tile("perm", [P, P], F32)
-        ident_b = keep_tile("ident_b", [P, P], BF16)
-        brow = keep_tile("brow", [P, P], BF16)
-        bias = keep_tile("bias", [P, K * NCC], F32)
+        bias = keep_tile("bias", [P, K, NCC], BF16)
         gsv = keep_tile("gsv", [P, 4], F32)
         s2b = keep_tile("s2b", [32, 1], BF16)
         s2v = keep_tile("s2v", [P, 1], F32)
         gain = keep_tile("gain", [P, C], BF16)
         shift = keep_tile("shift", [P, C], BF16)
         sums = keep_tile("sums", [P, B], F32)
-        nmean = keep_tile("nmean", [P, B], F32)
+        mean = keep_tile("mean", [P, B], F32)
         ssq = keep_tile("ssq", [P, B], F32)
         vare = keep_tile("vare", [P, B], F32)
         rstd = keep_tile("rstd", [P, B], F32)
@@ -74,42 +72,40 @@ def tile_block_attention_guide_pb_kernel(
         warm = keep_tile("warm", [P, 1], F32)
         zeros = keep_tile("zeros", [P, 512], BF16)
 
-        def tp_tile(dt=F32, n=512):
-            return psum.tile([P, n], dt, name="tp", bufs=TP_BANKS)
+        def tp_tile():
+            return psum.tile([P, 512], F32, name="tp", bufs=TP_BANKS)
 
         def mm_tile():
             return psum.tile([P, 512], F32, name="mm", bufs=8 - TP_BANKS)
 
-        g_src = g1_bytes.rearrange("b j c -> j b c")
-        w_src = conv2_w.rearrange("(k cc m) c -> cc m k c", k=K, cc=NCC)
+        g_src = g1_bytes.rearrange("(h j bb) (v e) c -> h (bb v) j (e c)", h=2, j=2, e=2)
+        w_src = conv2_w.rearrange("(k m f cc) c -> f k m cc c", k=K, m=P, f=2)
         r_src = res1.rearrange("b j c -> j b c")
 
-        def load_g(q):
-            nc.sync.dma_start(out=gb[q][:], in_=g_src[:, 2 * q : 2 * q + 2, :])
+        def load_g(h):
+            nc.sync.dma_start(out=gb[h][:].rearrange("p j e c -> p j (e c)"), in_=g_src[h])
 
         def load_w(j):
-            nc.sync.dma_start(out=wr[j][:], in_=w_src[j // 2][:, 2 * (j % 2) : 2 * (j % 2) + 2, :])
+            nc.sync.dma_start(out=wr[j][:], in_=w_src[j // 4][j % 4])
 
         def load_r(p):
             nc.sync.dma_start(out=res[p][:], in_=r_src[:, 2 * p : 2 * p + 2, :])
 
+        load_g(0)
         nc.vector.memset(zeros[:].bitcast(U32), 0)
         nc.vector.memset(warm[:], 0.0)
-        load_g(0)
-        load_w(0)
-        load_g(1)
         nc.scalar.dma_start(out=gsv[:], in_=g1_scale.rearrange("a b (p t) -> p (a b t)", t=4))
+        nc.scalar.dma_start(out=bias[:], in_=conv2_b.rearrange("(k m cc) -> m k cc", k=K, cc=NCC))
         nc.scalar.activation(out=warm[:], in_=warm[:], func=ACT.Square)
         make_identity(nc, ident[:])
-        nc.gpsimd.memset(brow[:], 0.0)
-        nc.scalar.dma_start(out=brow[0 : K * NCC, :], in_=conv2_b.rearrange("(r m) -> r m", m=P))
-        nc.scalar.dma_start(out=s2b[:], in_=s2.partition_broadcast(32))
         nc.gpsimd.memset(s2v[:], 1.0)
         nc.gpsimd.memset(mhalf[:], -0.5)
-        for j in range(1, 8):
+        for j in range(4):
             load_w(j)
-        load_g(2)
-        load_g(3)
+        nc.scalar.dma_start(out=s2b[:], in_=s2.partition_broadcast(32))
+        for j in range(4, 8):
+            load_w(j)
+        load_g(1)
         nc.sync.dma_start(out=a_raw[0:32, :, :, :], in_=adj.rearrange("b o (q t) w -> q b (o t w)", t=4))
         nc.sync.dma_start(
             out=a_raw[32:P, :, :, :].rearrange("p b t w -> p b (t w)"),
@@ -122,14 +118,11 @@ def tile_block_attention_guide_pb_kernel(
             load_r(p)
 
         nc.vector.tensor_copy(
-            out=perm[:].rearrange("p (u q e) -> p u q e", u=2, e=2),
-            in_=ident[:].rearrange("p (q u e) -> p u q e", u=2, e=2),
+            out=perm[:].rearrange("p (x u q) -> p x u q", x=2, u=2),
+            in_=ident[:].rearrange("p (x q u) -> p x u q", x=2, u=2),
         )
-        nc.vector.tensor_copy(out=ident_b[:], in_=ident[:])
 
         g_banks, w_banks, h_banks, t_banks, o_banks, x2s, ys = {}, {}, {}, {}, {}, {}, {}
-
-        b_bank = {}
 
         def either(on_vector):
             return nc.vector.tensor_copy if on_vector else nc.scalar.copy
@@ -139,40 +132,28 @@ def tile_block_attention_guide_pb_kernel(
             for r in range(n):
                 nc.tensor.matmul(out=bank[:], lhsT=zeros[:, 0:P], rhs=zeros[:], start=True, stop=True)
 
-        def bias_transpose():
-            b_bank[0] = tp_tile(BF16, P)
-            nc.tensor.transpose(b_bank[0][:], brow[:], ident_b[:])
+        def g_widen(h, j, on_vector):
+            either(on_vector)(out=gw[h][j][:], in_=gb[h][:, j, :, :].bitcast(FP8))
 
-        def bias_copy(on_vector):
-            either(on_vector)(out=bias[:], in_=b_bank[0][:, 0 : K * NCC])
-
-        def g_widen(q, on_vector):
-            either(on_vector)(out=gw[q][:], in_=gb[q][:].bitcast(FP8))
-
-        def g_transpose(q):
+        def g_transpose(h, e):
             bank = tp_tile()
-            g_banks[q] = bank
-            for bb in range(2):
-                words = gw[q][:, bb, :].bitcast(F32)
+            g_banks[(h, e)] = bank
+            for j in range(2):
+                words = gw[h][j][:, e, :].bitcast(F32)
                 for u in range(2):
-                    o = 256 * u + 128 * bb
+                    o = 256 * u + 128 * j
                     nc.tensor.transpose(bank[:, o : o + 128], words[:, u::2], perm[:])
 
-        def g_scale(q):
+        def g_scale(h, e):
             nc.vector.tensor_tensor(
-                out=gs[q][:].rearrange("p r (u e) -> p r u e", u=2),
-                in0=g_banks[q][:].bitcast(BF16).rearrange("p (u r e) -> p r u e", u=2, e=2),
+                out=gs[h][:, 256 * e : 256 * e + 256, :].rearrange("p r (u e) -> p r u e", u=2),
+                in0=g_banks[(h, e)][:].bitcast(BF16).rearrange("p (u r e) -> p r u e", u=2, e=2),
                 in1=gsv[:].rearrange("p (u e) -> p u e", u=2).unsqueeze(1).to_broadcast([P, 256, 2, 2]),
                 op=ALU.mult,
             )
 
-        group_of = [g for g, (b0, n) in enumerate(GROUPS) for q in range(n // 2)]
-
-        def g_quant(q):
-            g = group_of[q]
-            o = 2 * J * (q - GROUPS[g][0] // 2)
-            cols = slice(o, o + 2 * J)
-            nc.vector.quantize_mx(out=gc[g][:, cols].bitcast(FP8X4), scales=gsc[g][:, cols], in_=gs[q][:].rearrange("p r t -> p (r t)"))
+        def g_quant(h):
+            nc.vector.quantize_mx(out=gc[h][:].bitcast(FP8X4), scales=gsc[h][:], in_=gs[h][:].rearrange("p r t -> p (r t)"))
 
         def w_transpose(j):
             bank = tp_tile()
@@ -192,30 +173,30 @@ def tile_block_attention_guide_pb_kernel(
         def w_quant(j):
             nc.vector.quantize_mx(out=wc[j][:].bitcast(FP8X4), scales=wsc[j][:], in_=wi[j][:].rearrange("p m t -> p (m t)"))
 
-        def a_scale(p):
-            nc.gpsimd.tensor_scalar(
-                out=a_bf[p][:], in0=a_raw[:, 2 * p : 2 * p + 2, :, :].rearrange("p b t w -> p b w t"),
-                scalar1=s2v[:, 0:1], scalar2=0.0, op0=ALU.mult, op1=ALU.add,
-            )
+        def a_scale(p, on_vector):
+            src = a_raw[:, 2 * p : 2 * p + 2, :, :].rearrange("p b t w -> p b w t")
+            if on_vector:
+                nc.vector.tensor_scalar(out=a_bf[p][:], in0=src, scalar1=s2v[:, 0:1], scalar2=None, op0=ALU.mult)
+            else:
+                nc.scalar.activation(out=a_bf[p][:], in_=src, func=ACT.Copy, scale=s2v[:, 0:1])
 
         def a_quant(p):
             nc.vector.quantize_mx(out=ac[p][:].bitcast(FP8X4), scales=asc[p][:], in_=a_bf[p][:].rearrange("p b w t -> p (b w t)"))
 
-        def h_matmul(p, i, times=1):
-            j, cols = i // 2, slice(P * (i % 2), P * (i % 2) + P)
+        def h_matmul(h, k, cc, times=1):
+            j, cols = 4 * (cc // 2) + k, slice(P * (cc % 2), P * (cc % 2) + P)
             bank = mm_tile()
-            h_banks[(p, i)] = bank
+            h_banks[(h, k, cc)] = bank
             for r in range(times):
                 nc.tensor.matmul_mx(
-                    out=bank[:, 0 : J * GROUPS[p][1]], lhsT=wc[j][:, cols].bitcast(FP8X4), lhsT_scale=wsc[j][:, cols],
-                    rhs=gc[p][:].bitcast(FP8X4), rhs_scale=gsc[p][:], start=True, stop=True,
+                    out=bank[:], lhsT=wc[j][:, cols].bitcast(FP8X4), lhsT_scale=wsc[j][:, cols],
+                    rhs=gc[h][:].bitcast(FP8X4), rhs_scale=gsc[h][:], start=True, stop=True,
                 )
 
-        def h_bias(p, i, on_vector):
-            cc, k = i // K, i % K
-            out = hh[p][cc][:, :, k, :]
-            src = h_banks[(p, i)][:, 0 : J * GROUPS[p][1]].rearrange("p (x v) -> p x v", v=64)
-            col = bias[:, k * NCC + cc : k * NCC + cc + 1]
+        def h_bias(h, k, cc, on_vector):
+            out = hh[h][cc][:, :, k, :].rearrange("p x (q e) -> p x q e", e=2)
+            src = h_banks[(h, k, cc)][:].rearrange("p (e x q) -> p x q e", e=2, q=32)
+            col = bias[:, k, cc : cc + 1]
             if on_vector:
                 nc.vector.tensor_scalar(out=out, in0=src, scalar1=col, scalar2=None, op0=ALU.add)
             else:
@@ -224,9 +205,8 @@ def tile_block_attention_guide_pb_kernel(
         def h_transpose(p, cc):
             bank = tp_tile()
             t_banks[(p, cc)] = bank
-            g = group_of[p]
             for x in range(4):
-                words = hh[g][cc][:, 4 * (p - GROUPS[g][0] // 2) + x, :, :].rearrange("p k v -> p (k v)").bitcast(F32)
+                words = hh[p // 2][cc][:, 4 * (p % 2) + x, :, :].rearrange("p k v -> p (k v)").bitcast(F32)
                 nc.tensor.transpose(bank[:, 128 * x : 128 * x + 128], words, ident[:])
 
         def h_copy(p, cc, on_vector):
@@ -242,255 +222,255 @@ def tile_block_attention_guide_pb_kernel(
                 out=hc[p][f][:].bitcast(FP8X4), scales=hsc[p][f][:], in_=hq[p][f][:].rearrange("p b c t -> p (b c t)")
             )
 
-        def o_matmul(b, f):
+        def o_matmul(b):
             p, cols, half = b // 2, slice(J * (b % 2), J * (b % 2) + J), slice(256 * (b % 2), 256 * (b % 2) + 256)
-            if f == 0:
-                o_banks[b] = mm_tile()
-            nc.tensor.matmul_mx(
-                out=o_banks[b][:, 256 * f : 256 * f + 256], lhsT=ac[p][:, cols].bitcast(FP8X4), lhsT_scale=asc[p][:, cols],
-                rhs=hc[p][f][:, half].bitcast(FP8X4), rhs_scale=hsc[p][f][:, half], start=True, stop=True,
-            )
+            o_banks[b] = mm_tile()
+            for f in range(2):
+                nc.tensor.matmul_mx(
+                    out=o_banks[b][:, 256 * f : 256 * f + 256],
+                    lhsT=ac[p][:, cols].bitcast(FP8X4), lhsT_scale=asc[p][:, cols],
+                    rhs=hc[p][f][:, half].bitcast(FP8X4), rhs_scale=hsc[p][f][:, half], start=True, stop=True,
+                )
 
         def residual(b):
-            x2 = work.tile([P, C], F32, name="x2", bufs=4)
+            x2 = work.tile([P, C], F32, name="x2", bufs=8)
             x2s[b] = x2
             nc.vector.scalar_tensor_tensor(
-                out=x2[:], in0=o_banks[b][:], scalar=1.0, in1=res[b // 2][:, b % 2, :],
+                out=x2[:].rearrange("p (m c) -> p m c", c=NCC), in0=o_banks[b][:].rearrange("p (c m) -> p m c", c=NCC),
+                scalar=1.0, in1=res[b // 2][:, b % 2, :].rearrange("p (m c) -> p m c", c=NCC),
                 op0=ALU.mult, op1=ALU.add, accum_out=sums[:, b : b + 1],
             )
             nc.sync.dma_start(out=out_0[b], in_=x2[:])
             nc.gpsimd.tensor_scalar(
-                out=nmean[:, b : b + 1], in0=sums[:, b : b + 1], scalar1=-1.0 / C, scalar2=0.0, op0=ALU.mult, op1=ALU.add
+                out=mean[:, b : b + 1], in0=sums[:, b : b + 1], scalar1=1.0 / C, scalar2=0.0, op0=ALU.mult, op1=ALU.add
             )
 
         def variance(b):
             junk = work.tile([P, C], BF16, name="junk", bufs=2)
             nc.scalar.activation(
-                out=junk[:], in_=x2s[b][:], func=ACT.Square, bias=nmean[:, b : b + 1], accum_out=ssq[:, b : b + 1]
+                out=junk[:], in_=x2s[b][:], func=ACT.Square, scale=-float(C), bias=sums[:, b : b + 1],
+                accum_out=ssq[:, b : b + 1],
             )
             nc.gpsimd.tensor_scalar(
-                out=vare[:, b : b + 1], in0=ssq[:, b : b + 1], scalar1=1.0 / C, scalar2=EPS, op0=ALU.mult, op1=ALU.add
+                out=vare[:, b : b + 1], in0=ssq[:, b : b + 1], scalar1=1.0 / C**3, scalar2=EPS, op0=ALU.mult, op1=ALU.add
             )
             nc.gpsimd.tensor_tensor(out=rstd[:, b : b + 1], in0=vare[:, b : b + 1], in1=mhalf[:], op=ALU.pow)
 
         def centre(b):
-            y = work.tile([P, C], F32, name="y", bufs=3)
+            y = work.tile([P, C], F32, name="y", bufs=4)
             ys[b] = y
             nc.vector.scalar_tensor_tensor(
-                out=y[:], in0=x2s[b][:], scalar=nmean[:, b : b + 1], in1=gain[:], op0=ALU.add, op1=ALU.mult
+                out=y[:], in0=x2s[b][:], scalar=mean[:, b : b + 1], in1=gain[:], op0=ALU.subtract, op1=ALU.mult
             )
 
         def normalise(b):
-            xn = work.tile([P, C], F32, name="xn", bufs=3)
+            xn = work.tile([P, C], F32, name="xn", bufs=8)
             nc.vector.scalar_tensor_tensor(
                 out=xn[:], in0=ys[b][:], scalar=rstd[:, b : b + 1], in1=shift[:], op0=ALU.mult, op1=ALU.add
             )
             nc.sync.dma_start(out=out_1[b], in_=xn[:])
 
         nc.gpsimd.tensor_copy(out=s2v[0:32, :], in_=s2b[:])
-        warm_up(6)
-        g_widen(0, True)
+        warm_up(1)
+        warm_up(1)
+        warm_up(1)
+        warm_up(1)
+        warm_up(1)
+        warm_up(1)
+        g_widen(0, 0, True)
+        warm_up(1)
+        g_widen(0, 1, True)
         w_transpose(0)
-        g_widen(1, False)
-        warm_up(1)
+        g_transpose(0, 0)
         w_copy(0, True)
-        g_transpose(0)
+        warm_up(1)
+        g_scale(0, 0)
+        warm_up(1)
+        warm_up(1)
         w_quant(0)
-        g_transpose(1)
-        g_scale(0)
         warm_up(1)
-        bias_transpose()
-        g_scale(1)
+        g_transpose(0, 1)
         warm_up(1)
-        bias_copy(False)
+        g_scale(0, 1)
+        warm_up(1)
         w_transpose(1)
-        g_quant(0)
-        g_quant(1)
-        h_matmul(0, 0)
-        g_widen(2, True)
-        w_copy(1, False)
-        g_widen(3, True)
-        w_transpose(2)
-        h_bias(0, 0, True)
-        w_quant(1)
-        w_transpose(3)
-        w_copy(2, False)
-        a_scale(0)
-        w_quant(2)
-        h_matmul(0, 3)
-        w_copy(3, True)
-        h_matmul(0, 2)
-        w_quant(3)
-        a_scale(1)
-        h_bias(0, 3, True)
-        h_matmul(0, 1)
-        h_bias(0, 2, False)
-        w_transpose(4)
-        a_quant(0)
-        h_bias(0, 1, True)
-        h_matmul(0, 4)
-        a_scale(3)
-        w_copy(4, False)
-        a_quant(1)
-        h_matmul(0, 5)
-        h_transpose(1, 0)
-        h_bias(0, 4, False)
-        w_quant(4)
-        w_transpose(5)
-        a_scale(2)
-        h_copy(1, 0, True)
-        h_bias(0, 5, False)
-        h_matmul(0, 7)
-        w_copy(5, True)
-        h_matmul(0, 6)
         w_transpose(6)
-        h_bias(0, 7, True)
-        h_bias(0, 6, False)
-        h_matmul(0, 8)
-        w_quant(5)
+        g_quant(0)
+        w_copy(1, False)
+        w_transpose(4)
         w_copy(6, False)
-        h_transpose(1, 1)
-        a_quant(2)
-        h_bias(0, 8, True)
-        h_transpose(0, 1)
-        h_copy(1, 1, False)
-        h_matmul(0, 10)
+        g_widen(1, 1, True)
+        w_transpose(3)
+        w_quant(1)
+        w_transpose(2)
         w_quant(6)
-        h_matmul(0, 9)
-        h_copy(0, 1, False)
-        a_quant(3)
+        w_copy(3, False)
+        h_matmul(0, 1, 1)
+        w_copy(4, True)
+        w_copy(2, False)
+        w_quant(3)
+        w_transpose(5)
+        w_quant(4)
+        a_scale(0, False)
+        w_quant(2)
+        h_bias(0, 1, 1, True)
+        h_matmul(0, 0, 0)
+        a_scale(1, True)
+        a_scale(2, False)
+        h_matmul(0, 0, 1)
+        a_quant(0)
+        a_quant(1)
         w_transpose(7)
-        h_quant(1, 0)
-        h_bias(0, 9, False)
-        g_transpose(2)
-        h_bias(0, 10, True)
-        h_transpose(0, 0)
-        w_copy(7, True)
-        h_matmul(0, 13)
-        h_copy(0, 0, False)
-        h_matmul(0, 12, 2)
-        g_scale(2)
-        h_bias(0, 13, False)
-        g_transpose(3)
-        h_bias(0, 12, False)
+        g_widen(1, 0, True)
+        h_bias(0, 0, 0, False)
+        a_quant(2)
+        w_copy(5, False)
+        a_scale(3, True)
+        h_matmul(0, 2, 1)
+        h_bias(0, 0, 1, False)
+        h_matmul(0, 2, 0)
+        w_quant(5)
+        h_matmul(0, 1, 0)
+        w_copy(7, False)
+        a_quant(3)
+        h_matmul(0, 3, 1)
+        h_bias(0, 2, 0, True)
+        g_transpose(1, 1)
+        h_bias(0, 2, 1, False)
         w_quant(7)
-        h_matmul(0, 11)
+        g_transpose(1, 0)
+        h_bias(0, 1, 0, False)
+        g_scale(1, 1)
+        h_matmul(0, 1, 2)
+        h_bias(0, 3, 1, False)
+        h_matmul(0, 0, 2)
+        h_matmul(0, 3, 0)
+        h_bias(0, 1, 2, False)
+        h_matmul(0, 2, 3)
+        g_scale(1, 0)
+        h_transpose(0, 1)
+        h_transpose(1, 1)
+        h_bias(0, 0, 2, False)
+        h_bias(0, 2, 3, False)
+        h_matmul(0, 1, 3)
+        h_bias(0, 3, 0, True)
+        h_matmul(0, 0, 3)
+        h_copy(0, 1, False)
+        g_quant(1)
+        h_matmul(0, 3, 2)
+        h_transpose(0, 0)
+        h_transpose(1, 0)
+        h_copy(1, 1, False)
+        h_bias(0, 1, 3, True)
+        h_bias(0, 0, 3, False)
+        h_matmul(0, 2, 2, 2)
+        h_bias(0, 3, 2, True)
+        h_copy(0, 0, False)
+        h_matmul(0, 3, 3, 2)
+        h_copy(1, 0, False)
+        h_bias(0, 2, 2, True)
+        h_matmul(1, 0, 0, 2)
+        h_bias(0, 3, 3, False)
         h_quant(0, 0)
-        h_matmul(0, 14, 2)
-        h_bias(0, 11, False)
-        g_scale(3)
-        h_matmul(0, 15, 2)
-        h_bias(0, 14, False)
-        h_transpose(1, 2)
-        h_bias(0, 15, False)
+        h_matmul(1, 1, 1)
         h_transpose(0, 2)
-        g_quant(2)
-        g_quant(3)
-        h_copy(1, 2, False)
+        h_transpose(1, 2)
+        h_bias(1, 0, 0, False)
+        h_quant(1, 0)
+        h_bias(1, 1, 1, False)
         h_transpose(0, 3)
-        h_matmul(1, 2)
-        h_copy(0, 2, False)
-        h_copy(0, 3, True)
-        h_matmul(1, 7, 2)
-        h_bias(1, 2, False)
-        h_matmul(1, 3)
-        h_quant(0, 1)
-        h_matmul(1, 0)
-        h_bias(1, 3, False)
-        h_matmul(1, 1)
-        h_bias(1, 7, True)
-        o_matmul(0, 0)
-        o_matmul(0, 1)
-        h_bias(1, 0, False)
         h_transpose(1, 3)
-        residual(0)
-        o_matmul(1, 0)
-        o_matmul(1, 1)
-        h_bias(1, 1, False)
+        h_copy(0, 2, True)
+        h_copy(1, 2, False)
+        h_matmul(1, 0, 2)
         h_copy(1, 3, True)
-        h_matmul(1, 5)
-        variance(0)
-        h_matmul(1, 6)
-        residual(1)
-        h_transpose(3, 0)
-        h_bias(1, 5, False)
-        h_transpose(2, 0)
-        centre(0)
-        h_matmul(1, 4, 2)
-        h_bias(1, 6, False)
-        h_copy(2, 0, True)
-        h_matmul(1, 10)
-        variance(1)
-        centre(1)
-        h_matmul(1, 9)
-        h_matmul(1, 14)
-        h_bias(1, 4, False)
-        normalise(0)
-        h_matmul(1, 15)
-        h_bias(1, 9, False)
-        h_matmul(1, 11)
-        normalise(1)
-        h_transpose(2, 1)
-        h_bias(1, 10, False)
+        h_matmul(1, 1, 0)
+        h_matmul(1, 1, 2)
+        h_bias(1, 0, 2, False)
+        h_matmul(1, 2, 0, 2)
+        h_copy(0, 3, True)
+        h_bias(1, 1, 0, False)
+        h_matmul(1, 2, 1, 2)
         h_quant(1, 1)
-        h_bias(1, 11, False)
-        h_matmul(1, 8)
-        h_copy(2, 1, True)
-        o_matmul(2, 0)
-        o_matmul(2, 1)
-        h_copy(3, 0, False)
-        h_bias(1, 15, True)
-        h_bias(1, 14, False)
-        h_transpose(3, 1)
+        h_bias(1, 1, 2, False)
+        h_matmul(1, 3, 2, 2)
+        h_quant(0, 1)
+        h_bias(1, 2, 0, False)
+        o_matmul(2)
+        h_bias(1, 2, 1, True)
+        h_bias(1, 3, 2, False)
+        o_matmul(0)
         residual(2)
-        h_bias(1, 8, False)
-        h_matmul(1, 13)
-        h_quant(2, 0)
-        h_matmul(1, 12)
-        h_copy(3, 1, False)
-        h_transpose(3, 2)
-        centre(2)
-        h_bias(1, 12, False)
-        h_transpose(2, 2)
-        h_bias(1, 13, True)
-        o_matmul(3, 0)
-        o_matmul(3, 1)
+        o_matmul(3)
+        o_matmul(1)
+        residual(0)
+        h_matmul(1, 3, 0, 2)
         variance(2)
-        h_quant(3, 0)
-        h_transpose(2, 3)
-        h_copy(2, 2, False)
+        residual(1)
+        h_matmul(1, 3, 1, 2)
+        variance(0)
+        centre(0)
+        h_bias(1, 3, 0, False)
         residual(3)
-        h_copy(2, 3, False)
+        h_bias(1, 3, 1, False)
+        h_transpose(2, 0)
+        h_transpose(3, 0)
+        centre(1)
+        variance(1)
+        h_matmul(1, 0, 1, 2)
+        normalise(0)
+        variance(3)
+        h_matmul(1, 2, 2)
+        h_copy(3, 0, True)
+        h_matmul(1, 0, 3)
+        h_bias(1, 0, 1, False)
+        h_matmul(1, 2, 3, 2)
+        normalise(1)
+        h_bias(1, 0, 3, False)
+        h_matmul(1, 3, 3, 2)
+        h_bias(1, 2, 2, True)
+        h_bias(1, 2, 3, False)
+        h_transpose(2, 1)
+        h_transpose(3, 1)
+        h_copy(2, 0, True)
+        h_bias(1, 3, 3, False)
+        centre(2)
+        h_matmul(1, 1, 3)
+        h_copy(3, 1, False)
+        h_transpose(2, 2)
+        h_transpose(3, 2)
+        h_copy(2, 1, True)
+        h_bias(1, 1, 3, False)
         normalise(2)
         h_copy(3, 2, False)
-        centre(3)
-        variance(3)
+        h_quant(2, 0)
+        h_transpose(2, 3)
         h_transpose(3, 3)
-        h_quant(2, 1)
+        h_copy(2, 2, False)
+        h_quant(3, 0)
         h_copy(3, 3, False)
-        o_matmul(4, 0)
-        o_matmul(4, 1)
-        normalise(3)
-        o_matmul(5, 0)
-        o_matmul(5, 1)
+        centre(3)
+        h_copy(2, 3, False)
         h_quant(3, 1)
-        residual(5)
-        o_matmul(6, 0)
-        o_matmul(6, 1)
-        residual(4)
-        o_matmul(7, 0)
-        o_matmul(7, 1)
-        variance(5)
-        centre(5)
-        variance(4)
-        centre(4)
-        normalise(5)
+        h_quant(2, 1)
+        o_matmul(7)
+        normalise(3)
+        o_matmul(5)
         residual(7)
-        residual(6)
+        o_matmul(4)
+        residual(5)
         variance(7)
         centre(7)
+        o_matmul(6)
+        variance(5)
+        residual(4)
+        residual(6)
+        variance(4)
+        centre(4)
         variance(6)
-        centre(6)
+        centre(5)
         normalise(7)
-        normalise(6)
+        normalise(5)
+        centre(6)
         normalise(4)
+        normalise(6)

@@ -21,7 +21,7 @@ EPS = 1e-5
 
 FLOPS = 2 * B * J * C * K * C + 2 * B * K * J * J * C
 
-TP_BANKS = 4
+TP_BANKS = 3
 
 
 def tile_block_attention_guide_pb_kernel(
@@ -66,9 +66,8 @@ def tile_block_attention_guide_pb_kernel(
         sums = keep_tile("sums", [P, B], F32)
         mean = keep_tile("mean", [P, B], F32)
         ssq = keep_tile("ssq", [P, B], F32)
-        vare = keep_tile("vare", [P, B], F32)
         rstd = keep_tile("rstd", [P, B], F32)
-        mhalf = keep_tile("mhalf", [P, 1], F32)
+        eps = keep_tile("eps", [P, 1], F32)
         warm = keep_tile("warm", [P, 1], F32)
         zeros = keep_tile("zeros", [P, 512], BF16)
 
@@ -96,10 +95,10 @@ def tile_block_attention_guide_pb_kernel(
         nc.vector.memset(warm[:], 0.0)
         nc.scalar.dma_start(out=gsv[:], in_=g1_scale.rearrange("a b (p t) -> p (a b t)", t=4))
         nc.scalar.dma_start(out=bias[:], in_=conv2_b.rearrange("(k m cc) -> m k cc", k=K, cc=NCC))
-        nc.scalar.activation(out=warm[:], in_=warm[:], func=ACT.Square)
+        nc.vector.tensor_scalar(out=eps[:], in0=warm[:], scalar1=EPS, scalar2=None, op0=ALU.add)
+        nc.scalar.activation(out=warm[:], in_=eps[:], func=ACT.Abs_reciprocal_sqrt)
         make_identity(nc, ident[:])
         nc.gpsimd.memset(s2v[:], 1.0)
-        nc.gpsimd.memset(mhalf[:], -0.5)
         for j in range(4):
             load_w(j)
         nc.scalar.dma_start(out=s2b[:], in_=s2.partition_broadcast(32))
@@ -241,9 +240,9 @@ def tile_block_attention_guide_pb_kernel(
                 op0=ALU.mult, op1=ALU.add, accum_out=sums[:, b : b + 1],
             )
             nc.sync.dma_start(out=out_0[b], in_=x2[:])
-            nc.gpsimd.tensor_scalar(
-                out=mean[:, b : b + 1], in0=sums[:, b : b + 1], scalar1=1.0 / C, scalar2=0.0, op0=ALU.mult, op1=ALU.add
-            )
+
+        def average(b):
+            nc.scalar.activation(out=mean[:, b : b + 1], in_=sums[:, b : b + 1], func=ACT.Copy, scale=1.0 / C)
 
         def variance(b):
             junk = work.tile([P, C], BF16, name="junk", bufs=2)
@@ -251,10 +250,11 @@ def tile_block_attention_guide_pb_kernel(
                 out=junk[:], in_=x2s[b][:], func=ACT.Square, scale=-float(C), bias=sums[:, b : b + 1],
                 accum_out=ssq[:, b : b + 1],
             )
-            nc.gpsimd.tensor_scalar(
-                out=vare[:, b : b + 1], in0=ssq[:, b : b + 1], scalar1=1.0 / C**3, scalar2=EPS, op0=ALU.mult, op1=ALU.add
+
+        def deviation(b):
+            nc.scalar.activation(
+                out=rstd[:, b : b + 1], in_=ssq[:, b : b + 1], func=ACT.Abs_reciprocal_sqrt, scale=1.0 / C**3, bias=eps[:, 0:1]
             )
-            nc.gpsimd.tensor_tensor(out=rstd[:, b : b + 1], in0=vare[:, b : b + 1], in1=mhalf[:], op=ALU.pow)
 
         def centre(b):
             y = work.tile([P, C], F32, name="y", bufs=4)
@@ -277,200 +277,216 @@ def tile_block_attention_guide_pb_kernel(
         warm_up(1)
         warm_up(1)
         warm_up(1)
-        g_widen(0, 0, True)
         warm_up(1)
-        g_widen(0, 1, True)
+        g_widen(0, 0, False)
         w_transpose(0)
-        g_transpose(0, 0)
+        g_widen(0, 1, False)
+        warm_up(1)
+        warm_up(1)
         w_copy(0, True)
-        warm_up(1)
-        g_scale(0, 0)
-        warm_up(1)
-        warm_up(1)
+        w_transpose(1)
         w_quant(0)
-        warm_up(1)
         g_transpose(0, 1)
+        w_copy(1, True)
+        warm_up(1)
         warm_up(1)
         g_scale(0, 1)
+        g_transpose(0, 0)
         warm_up(1)
-        w_transpose(1)
-        w_transpose(6)
-        g_quant(0)
-        w_copy(1, False)
-        w_transpose(4)
-        w_copy(6, False)
-        g_widen(1, 1, True)
-        w_transpose(3)
         w_quant(1)
+        warm_up(1)
+        g_scale(0, 0)
+        w_transpose(4)
+        w_transpose(6)
+        w_copy(4, False)
         w_transpose(2)
-        w_quant(6)
-        w_copy(3, False)
-        h_matmul(0, 1, 1)
-        w_copy(4, True)
-        w_copy(2, False)
-        w_quant(3)
-        w_transpose(5)
+        g_quant(0)
+        w_copy(6, False)
+        w_transpose(3)
         w_quant(4)
-        a_scale(0, False)
-        w_quant(2)
-        h_bias(0, 1, 1, True)
-        h_matmul(0, 0, 0)
-        a_scale(1, True)
-        a_scale(2, False)
+        w_copy(2, True)
+        g_widen(1, 1, False)
         h_matmul(0, 0, 1)
-        a_quant(0)
-        a_quant(1)
-        w_transpose(7)
+        w_quant(6)
+        h_matmul(0, 0, 0)
+        w_quant(2)
+        w_copy(3, True)
+        h_matmul(0, 1, 0)
         g_widen(1, 0, True)
         h_bias(0, 0, 0, False)
-        a_quant(2)
-        w_copy(5, False)
-        a_scale(3, True)
-        h_matmul(0, 2, 1)
-        h_bias(0, 0, 1, False)
-        h_matmul(0, 2, 0)
-        w_quant(5)
-        h_matmul(0, 1, 0)
-        w_copy(7, False)
-        a_quant(3)
-        h_matmul(0, 3, 1)
-        h_bias(0, 2, 0, True)
-        g_transpose(1, 1)
-        h_bias(0, 2, 1, False)
-        w_quant(7)
-        g_transpose(1, 0)
+        w_transpose(5)
+        w_quant(3)
         h_bias(0, 1, 0, False)
-        g_scale(1, 1)
-        h_matmul(0, 1, 2)
-        h_bias(0, 3, 1, False)
-        h_matmul(0, 0, 2)
+        w_transpose(7)
+        h_bias(0, 0, 1, True)
+        w_copy(5, False)
+        h_matmul(0, 1, 1)
+        a_scale(0, True)
         h_matmul(0, 3, 0)
-        h_bias(0, 1, 2, False)
-        h_matmul(0, 2, 3)
-        g_scale(1, 0)
-        h_transpose(0, 1)
-        h_transpose(1, 1)
-        h_bias(0, 0, 2, False)
-        h_bias(0, 2, 3, False)
+        w_copy(7, False)
+        h_matmul(0, 3, 1, 2)
+        w_quant(5)
+        h_bias(0, 1, 1, False)
+        g_transpose(1, 1)
+        a_quant(0)
+        w_quant(7)
+        h_bias(0, 3, 0, False)
         h_matmul(0, 1, 3)
-        h_bias(0, 3, 0, True)
+        a_scale(1, True)
+        h_bias(0, 3, 1, False)
+        h_matmul(0, 2, 0)
+        g_transpose(1, 0)
+        g_scale(1, 1)
+        h_bias(0, 1, 3, False)
+        h_matmul(0, 2, 1)
+        h_bias(0, 2, 0, False)
         h_matmul(0, 0, 3)
-        h_copy(0, 1, False)
-        g_quant(1)
-        h_matmul(0, 3, 2)
+        a_quant(1)
+        h_matmul(0, 1, 2, 2)
+        a_scale(2, False)
+        h_bias(0, 2, 1, True)
         h_transpose(0, 0)
         h_transpose(1, 0)
-        h_copy(1, 1, False)
-        h_bias(0, 1, 3, True)
+        g_scale(1, 0)
+        h_matmul(0, 0, 2)
         h_bias(0, 0, 3, False)
-        h_matmul(0, 2, 2, 2)
-        h_bias(0, 3, 2, True)
-        h_copy(0, 0, False)
-        h_matmul(0, 3, 3, 2)
-        h_copy(1, 0, False)
-        h_bias(0, 2, 2, True)
-        h_matmul(1, 0, 0, 2)
+        h_matmul(0, 2, 2)
+        h_copy(0, 0, True)
+        h_matmul(0, 2, 3)
+        h_bias(0, 1, 2, False)
+        h_matmul(0, 3, 3)
+        a_quant(2)
+        h_bias(0, 0, 2, False)
+        h_transpose(0, 1)
+        h_transpose(1, 1)
+        g_quant(1)
         h_bias(0, 3, 3, False)
+        h_matmul(0, 3, 2, 2)
+        h_bias(0, 2, 3, True)
+        h_bias(0, 2, 2, False)
+        h_copy(0, 1, True)
+        h_matmul(1, 0, 0)
+        h_copy(1, 1, False)
+        h_matmul(1, 1, 1, 2)
+        h_copy(1, 0, True)
+        h_bias(0, 3, 2, False)
+        h_matmul(1, 0, 1)
         h_quant(0, 0)
-        h_matmul(1, 1, 1)
-        h_transpose(0, 2)
-        h_transpose(1, 2)
+        h_matmul(1, 2, 0)
         h_bias(1, 0, 0, False)
-        h_quant(1, 0)
-        h_bias(1, 1, 1, False)
         h_transpose(0, 3)
         h_transpose(1, 3)
-        h_copy(0, 2, True)
-        h_copy(1, 2, False)
-        h_matmul(1, 0, 2)
-        h_copy(1, 3, True)
-        h_matmul(1, 1, 0)
+        h_quant(1, 0)
+        h_bias(1, 1, 1, False)
         h_matmul(1, 1, 2)
-        h_bias(1, 0, 2, False)
-        h_matmul(1, 2, 0, 2)
-        h_copy(0, 3, True)
-        h_bias(1, 1, 0, False)
-        h_matmul(1, 2, 1, 2)
-        h_quant(1, 1)
-        h_bias(1, 1, 2, False)
-        h_matmul(1, 3, 2, 2)
-        h_quant(0, 1)
-        h_bias(1, 2, 0, False)
-        o_matmul(2)
-        h_bias(1, 2, 1, True)
-        h_bias(1, 3, 2, False)
-        o_matmul(0)
-        residual(2)
-        o_matmul(3)
-        o_matmul(1)
-        residual(0)
-        h_matmul(1, 3, 0, 2)
-        variance(2)
-        residual(1)
-        h_matmul(1, 3, 1, 2)
-        variance(0)
-        centre(0)
-        h_bias(1, 3, 0, False)
-        residual(3)
-        h_bias(1, 3, 1, False)
-        h_transpose(2, 0)
-        h_transpose(3, 0)
-        centre(1)
-        variance(1)
-        h_matmul(1, 0, 1, 2)
-        normalise(0)
-        variance(3)
-        h_matmul(1, 2, 2)
-        h_copy(3, 0, True)
-        h_matmul(1, 0, 3)
+        h_bias(1, 2, 0, True)
         h_bias(1, 0, 1, False)
-        h_matmul(1, 2, 3, 2)
-        normalise(1)
-        h_bias(1, 0, 3, False)
+        h_matmul(1, 2, 1)
+        h_copy(0, 3, True)
+        h_matmul(1, 3, 1, 2)
+        h_bias(1, 1, 2, False)
+        h_matmul(1, 3, 0)
+        a_scale(3, True)
+        h_transpose(0, 2)
+        h_transpose(1, 2)
+        h_bias(1, 2, 1, False)
+        h_copy(1, 3, True)
+        h_bias(1, 3, 0, False)
+        h_matmul(1, 0, 2)
+        a_quant(3)
+        h_matmul(1, 1, 0)
+        h_bias(1, 3, 1, False)
+        h_copy(0, 2, True)
         h_matmul(1, 3, 3, 2)
-        h_bias(1, 2, 2, True)
-        h_bias(1, 2, 3, False)
+        h_copy(1, 2, False)
+        h_bias(1, 1, 0, True)
+        h_matmul(1, 1, 3)
         h_transpose(2, 1)
         h_transpose(3, 1)
-        h_copy(2, 0, True)
-        h_bias(1, 3, 3, False)
-        centre(2)
-        h_matmul(1, 1, 3)
+        h_bias(1, 0, 2, False)
+        h_quant(0, 1)
+        h_bias(1, 1, 3, False)
+        h_matmul(1, 0, 3)
+        h_quant(1, 1)
+        o_matmul(0)
         h_copy(3, 1, False)
+        o_matmul(1)
+        h_bias(1, 3, 3, True)
+        h_copy(2, 1, False)
+        residual(0)
+        o_matmul(2)
+        h_bias(1, 0, 3, False)
+        residual(1)
+        o_matmul(3)
+        variance(0)
+        h_transpose(2, 0)
+        h_transpose(3, 0)
+        residual(2)
+        average(0)
+        variance(1)
+        h_matmul(1, 3, 2)
+        centre(0)
+        h_matmul(1, 2, 2, 2)
+        average(2)
+        deviation(0)
+        variance(2)
+        h_copy(2, 0, True)
+        h_matmul(1, 2, 3)
+        deviation(1)
+        h_bias(1, 2, 2, True)
+        h_bias(1, 3, 2, False)
+        normalise(0)
+        h_bias(1, 2, 3, False)
         h_transpose(2, 2)
         h_transpose(3, 2)
-        h_copy(2, 1, True)
-        h_bias(1, 1, 3, False)
-        normalise(2)
-        h_copy(3, 2, False)
         h_quant(2, 0)
-        h_transpose(2, 3)
-        h_transpose(3, 3)
+        deviation(2)
+        average(1)
+        h_copy(3, 0, False)
+        centre(1)
         h_copy(2, 2, False)
         h_quant(3, 0)
+        h_copy(3, 2, False)
+        h_transpose(2, 3)
+        h_transpose(3, 3)
+        normalise(1)
+        residual(3)
         h_copy(3, 3, False)
-        centre(3)
+        centre(2)
         h_copy(2, 3, False)
         h_quant(3, 1)
+        variance(3)
         h_quant(2, 1)
-        o_matmul(7)
-        normalise(3)
-        o_matmul(5)
-        residual(7)
-        o_matmul(4)
-        residual(5)
-        variance(7)
-        centre(7)
+        average(3)
         o_matmul(6)
-        variance(5)
-        residual(4)
+        deviation(3)
+        centre(3)
+        o_matmul(4)
+        normalise(2)
+        normalise(3)
+        o_matmul(7)
         residual(6)
-        variance(4)
-        centre(4)
+        o_matmul(5)
+        residual(4)
+        average(6)
         variance(6)
-        centre(5)
-        normalise(7)
-        normalise(5)
         centre(6)
-        normalise(4)
+        variance(4)
+        residual(5)
+        deviation(6)
+        average(4)
+        deviation(4)
+        residual(7)
+        average(5)
+        variance(5)
+        centre(4)
+        variance(7)
         normalise(6)
+        deviation(5)
+        average(7)
+        deviation(7)
+        normalise(4)
+        centre(5)
+        centre(7)
+        normalise(5)
+        normalise(7)

@@ -14,7 +14,6 @@ ACT = mybir.ActivationFunctionType
 
 B, J, C, K = 8, 128, 512, 4
 P = 128
-HALF = 4
 PAIRS = B // 2
 NCC = C // P
 EPS = 1e-5
@@ -22,6 +21,7 @@ EPS = 1e-5
 FLOPS = 2 * B * J * C * K * C + 2 * B * K * J * J * C
 
 TP_BANKS = 3
+GROUPS = ((0, 1), (2,), (3,))
 
 
 def tile_block_attention_guide_pb_kernel(
@@ -37,26 +37,28 @@ def tile_block_attention_guide_pb_kernel(
         def keep_tile(name, shape, dt):
             return keep.tile(shape, dt, name=name, align_bytes=64)
 
-        gb = [keep_tile("gb%d" % h, [P, 2, 2, C], U8) for h in range(2)]
-        gw = [[keep_tile("gw%d_%d" % (h, j), [P, 2, C], BF16) for j in range(2)] for h in range(2)]
-        gs = [keep_tile("gs%d" % h, [P, HALF * J, 4], BF16) for h in range(2)]
-        gc = [keep_tile("gc%d" % h, [P, HALF * J], U32) for h in range(2)]
-        gsc = [keep_tile("gsc%d" % h, [P, HALF * J], U8) for h in range(2)]
+        sizes = [len(pairs) for pairs in GROUPS]
+        gb = [keep_tile("gb%d" % p, [P, 2, C], U8) for p in range(PAIRS)]
+        gw = [keep_tile("gw%d" % p, [P, 2, C], BF16) for p in range(PAIRS)]
+        gs = [keep_tile("gs%d" % g, [P, 2 * J * n, 4], BF16) for g, n in enumerate(sizes)]
+        gc = [keep_tile("gc%d" % g, [P, 2 * J * n], U32) for g, n in enumerate(sizes)]
+        gsc = [keep_tile("gsc%d" % g, [P, 2 * J * n], U8) for g, n in enumerate(sizes)]
         wr = [keep_tile("wr%d" % j, [P, 2, C], BF16) for j in range(8)]
         wi = [keep_tile("wi%d" % j, [P, 2 * P, 4], BF16) for j in range(8)]
         wc = [keep_tile("wc%d" % j, [P, 2 * P], U32) for j in range(8)]
         wsc = [keep_tile("wsc%d" % j, [P, 2 * P], U8) for j in range(8)]
-        hh = [[keep_tile("hh%d_%d" % (h, cc), [P, 2 * HALF, K, J // 2], BF16) for cc in range(NCC)] for h in range(2)]
+        hh = [[keep_tile("hh%d_%d" % (g, cc), [P, 4 * n, K, J // 2], BF16) for cc in range(NCC)] for g, n in enumerate(sizes)]
         hq = [[keep_tile("hq%d_%d" % (p, f), [P, 2, C // 2, 4], BF16) for f in range(2)] for p in range(PAIRS)]
         hc = [[keep_tile("hc%d_%d" % (p, f), [P, C], U32) for f in range(2)] for p in range(PAIRS)]
         hsc = [[keep_tile("hsc%d_%d" % (p, f), [P, C], U8) for f in range(2)] for p in range(PAIRS)]
-        a_raw = keep_tile("a_raw", [P, B, 4, J], BF16)
+        a_raw = [keep_tile("a_raw%d" % p, [P, 2, 4, J], BF16) for p in range(PAIRS)]
         a_bf = [keep_tile("a_bf%d" % p, [P, 2, J, 4], BF16) for p in range(PAIRS)]
         ac = [keep_tile("ac%d" % p, [P, 2 * J], U32) for p in range(PAIRS)]
         asc = [keep_tile("asc%d" % p, [P, 2 * J], U8) for p in range(PAIRS)]
         res = [keep_tile("res%d" % p, [P, 2, C], BF16) for p in range(PAIRS)]
         ident = keep_tile("ident", [P, P], F32)
         perm = keep_tile("perm", [P, P], F32)
+        ident_b = keep_tile("ident_b", [P, P], BF16)
         bias = keep_tile("bias", [P, K, NCC], BF16)
         gsv = keep_tile("gsv", [P, 4], F32)
         s2b = keep_tile("s2b", [32, 1], BF16)
@@ -77,39 +79,48 @@ def tile_block_attention_guide_pb_kernel(
         def mm_tile():
             return psum.tile([P, 512], F32, name="mm", bufs=8 - TP_BANKS)
 
-        g_src = g1_bytes.rearrange("(h j bb) (v e) c -> h (bb v) j (e c)", h=2, j=2, e=2)
+        g_src = g1_bytes.rearrange("(p bb) (v e) c -> p (bb v) (e c)", bb=2, e=2)
         w_src = conv2_w.rearrange("(k m f cc) c -> f k m cc c", k=K, m=P, f=2)
         r_src = res1.rearrange("b j c -> j b c")
 
-        def load_g(h):
-            nc.sync.dma_start(out=gb[h][:].rearrange("p j e c -> p j (e c)"), in_=g_src[h])
+        def load_g(p):
+            nc.sync.dma_start(out=gb[p][:].rearrange("p e c -> p (e c)"), in_=g_src[p])
 
         def load_w(j):
             nc.sync.dma_start(out=wr[j][:], in_=w_src[j // 4][j % 4])
 
+        adj_src = adj.rearrange("b o (q t) w -> q b (o t w)", t=4)
+        spatial_src = spatial_adj.rearrange("k (q t) w -> (k q) (t w)", t=4).unsqueeze(1).to_broadcast([96, 2, 4 * J])
+
+        def load_a(p):
+            nc.sync.dma_start(out=a_raw[p][0:32, :, :, :].rearrange("p b t w -> p b (t w)"), in_=adj_src[:, 2 * p : 2 * p + 2, :])
+            nc.sync.dma_start(out=a_raw[p][32:P, :, :, :].rearrange("p b t w -> p b (t w)"), in_=spatial_src)
+
         def load_r(p):
             nc.sync.dma_start(out=res[p][:], in_=r_src[:, 2 * p : 2 * p + 2, :])
 
-        load_g(0)
+        for p in GROUPS[0]:
+            load_g(p)
         nc.vector.memset(zeros[:].bitcast(U32), 0)
         nc.vector.memset(warm[:], 0.0)
         nc.scalar.dma_start(out=gsv[:], in_=g1_scale.rearrange("a b (p t) -> p (a b t)", t=4))
+        nc.scalar.dma_start(out=s2b[:], in_=s2.partition_broadcast(32))
         nc.scalar.dma_start(out=bias[:], in_=conv2_b.rearrange("(k m cc) -> m k cc", k=K, cc=NCC))
         nc.vector.tensor_scalar(out=eps[:], in0=warm[:], scalar1=EPS, scalar2=None, op0=ALU.add)
         nc.scalar.activation(out=warm[:], in_=eps[:], func=ACT.Abs_reciprocal_sqrt)
         make_identity(nc, ident[:])
         nc.gpsimd.memset(s2v[:], 1.0)
-        for j in range(4):
+        load_w(0)
+        load_w(1)
+        for p in range(len(GROUPS[0]), PAIRS):
+            load_g(p)
+        load_a(0)
+        load_w(2)
+        load_a(1)
+        for j in range(3, 8):
             load_w(j)
-        nc.scalar.dma_start(out=s2b[:], in_=s2.partition_broadcast(32))
-        for j in range(4, 8):
-            load_w(j)
-        load_g(1)
-        nc.sync.dma_start(out=a_raw[0:32, :, :, :], in_=adj.rearrange("b o (q t) w -> q b (o t w)", t=4))
-        nc.sync.dma_start(
-            out=a_raw[32:P, :, :, :].rearrange("p b t w -> p b (t w)"),
-            in_=spatial_adj.rearrange("k (q t) w -> (k q) (t w)", t=4).unsqueeze(1).to_broadcast([96, B, 512]),
-        )
+        load_a(2)
+        load_a(3)
         load_r(0)
         nc.sync.dma_start(out=gain[:], in_=norm2_g.partition_broadcast(P))
         nc.sync.dma_start(out=shift[:], in_=norm2_b.partition_broadcast(P))
@@ -121,7 +132,9 @@ def tile_block_attention_guide_pb_kernel(
             in_=ident[:].rearrange("p (x q u) -> p x u q", x=2, u=2),
         )
 
-        g_banks, w_banks, h_banks, t_banks, o_banks, x2s, ys = {}, {}, {}, {}, {}, {}, {}
+        nc.vector.tensor_copy(out=ident_b[:], in_=ident[:])
+
+        g_banks, w_banks, h_banks, t_banks, o_banks, n_banks, x2s, ys, diags, xns = {}, {}, {}, {}, {}, {}, {}, {}, {}, {}
 
         def either(on_vector):
             return nc.vector.tensor_copy if on_vector else nc.scalar.copy
@@ -131,28 +144,33 @@ def tile_block_attention_guide_pb_kernel(
             for r in range(n):
                 nc.tensor.matmul(out=bank[:], lhsT=zeros[:, 0:P], rhs=zeros[:], start=True, stop=True)
 
-        def g_widen(h, j, on_vector):
-            either(on_vector)(out=gw[h][j][:], in_=gb[h][:, j, :, :].bitcast(FP8))
+        def hot(j):
+            bank = mm_tile()
+            nc.tensor.matmul(out=bank[:], lhsT=zeros[:, 0:P], rhs=wr[j][:, 0, :], start=True, stop=True)
 
-        def g_transpose(h, e):
+        def g_widen(p, on_vector):
+            either(on_vector)(out=gw[p][:], in_=gb[p][:].bitcast(FP8))
+
+        def g_transpose(g, s):
             bank = tp_tile()
-            g_banks[(h, e)] = bank
-            for j in range(2):
-                words = gw[h][j][:, e, :].bitcast(F32)
+            g_banks[(g, s)] = bank
+            parts = [(p, s) for p in GROUPS[g]] if sizes[g] == 2 else [(GROUPS[g][0], e) for e in range(2)]
+            for y, (p, e) in enumerate(parts):
+                words = gw[p][:, e, :].bitcast(F32)
                 for u in range(2):
-                    o = 256 * u + 128 * j
+                    o = 256 * u + 128 * y
                     nc.tensor.transpose(bank[:, o : o + 128], words[:, u::2], perm[:])
 
-        def g_scale(h, e):
+        def g_scale(g, s):
             nc.vector.tensor_tensor(
-                out=gs[h][:, 256 * e : 256 * e + 256, :].rearrange("p r (u e) -> p r u e", u=2),
-                in0=g_banks[(h, e)][:].bitcast(BF16).rearrange("p (u r e) -> p r u e", u=2, e=2),
+                out=gs[g][:, 256 * s : 256 * s + 256, :].rearrange("p r (u e) -> p r u e", u=2),
+                in0=g_banks[(g, s)][:].bitcast(BF16).rearrange("p (u r e) -> p r u e", u=2, e=2),
                 in1=gsv[:].rearrange("p (u e) -> p u e", u=2).unsqueeze(1).to_broadcast([P, 256, 2, 2]),
                 op=ALU.mult,
             )
 
-        def g_quant(h):
-            nc.vector.quantize_mx(out=gc[h][:].bitcast(FP8X4), scales=gsc[h][:], in_=gs[h][:].rearrange("p r t -> p (r t)"))
+        def g_quant(g):
+            nc.vector.quantize_mx(out=gc[g][:].bitcast(FP8X4), scales=gsc[g][:], in_=gs[g][:].rearrange("p r t -> p (r t)"))
 
         def w_transpose(j):
             bank = tp_tile()
@@ -173,7 +191,7 @@ def tile_block_attention_guide_pb_kernel(
             nc.vector.quantize_mx(out=wc[j][:].bitcast(FP8X4), scales=wsc[j][:], in_=wi[j][:].rearrange("p m t -> p (m t)"))
 
         def a_scale(p, on_vector):
-            src = a_raw[:, 2 * p : 2 * p + 2, :, :].rearrange("p b t w -> p b w t")
+            src = a_raw[p][:].rearrange("p b t w -> p b w t")
             if on_vector:
                 nc.vector.tensor_scalar(out=a_bf[p][:], in0=src, scalar1=s2v[:, 0:1], scalar2=None, op0=ALU.mult)
             else:
@@ -183,18 +201,18 @@ def tile_block_attention_guide_pb_kernel(
             nc.vector.quantize_mx(out=ac[p][:].bitcast(FP8X4), scales=asc[p][:], in_=a_bf[p][:].rearrange("p b w t -> p (b w t)"))
 
         def h_matmul(h, k, cc, times=1):
-            j, cols = 4 * (cc // 2) + k, slice(P * (cc % 2), P * (cc % 2) + P)
+            j, cols, n = 4 * (cc // 2) + k, slice(P * (cc % 2), P * (cc % 2) + P), 2 * J * sizes[h]
             bank = mm_tile()
             h_banks[(h, k, cc)] = bank
             for r in range(times):
                 nc.tensor.matmul_mx(
-                    out=bank[:], lhsT=wc[j][:, cols].bitcast(FP8X4), lhsT_scale=wsc[j][:, cols],
+                    out=bank[:, 0:n], lhsT=wc[j][:, cols].bitcast(FP8X4), lhsT_scale=wsc[j][:, cols],
                     rhs=gc[h][:].bitcast(FP8X4), rhs_scale=gsc[h][:], start=True, stop=True,
                 )
 
         def h_bias(h, k, cc, on_vector):
             out = hh[h][cc][:, :, k, :].rearrange("p x (q e) -> p x q e", e=2)
-            src = h_banks[(h, k, cc)][:].rearrange("p (e x q) -> p x q e", e=2, q=32)
+            src = h_banks[(h, k, cc)][:, 0 : 2 * J * sizes[h]].rearrange("p (e x q) -> p x q e", e=2, q=32)
             col = bias[:, k, cc : cc + 1]
             if on_vector:
                 nc.vector.tensor_scalar(out=out, in0=src, scalar1=col, scalar2=None, op0=ALU.add)
@@ -204,8 +222,9 @@ def tile_block_attention_guide_pb_kernel(
         def h_transpose(p, cc):
             bank = tp_tile()
             t_banks[(p, cc)] = bank
+            g = [p in pairs for pairs in GROUPS].index(True)
             for x in range(4):
-                words = hh[p // 2][cc][:, 4 * (p % 2) + x, :, :].rearrange("p k v -> p (k v)").bitcast(F32)
+                words = hh[g][cc][:, 4 * GROUPS[g].index(p) + x, :, :].rearrange("p k v -> p (k v)").bitcast(F32)
                 nc.tensor.transpose(bank[:, 128 * x : 128 * x + 128], words, ident[:])
 
         def h_copy(p, cc, on_vector):
@@ -257,7 +276,7 @@ def tile_block_attention_guide_pb_kernel(
             )
 
         def centre(b):
-            y = work.tile([P, C], F32, name="y", bufs=4)
+            y = work.tile([P, C], F32, name="y", bufs=8)
             ys[b] = y
             nc.vector.scalar_tensor_tensor(
                 out=y[:], in0=x2s[b][:], scalar=mean[:, b : b + 1], in1=gain[:], op0=ALU.subtract, op1=ALU.mult
@@ -270,6 +289,31 @@ def tile_block_attention_guide_pb_kernel(
             )
             nc.sync.dma_start(out=out_1[b], in_=xn[:])
 
+        def normalise_part(b, s):
+            if b not in xns:
+                xns[b] = work.tile([P, C], F32, name="xn", bufs=8)
+            cols = slice(256 * s, 256 * s + 256)
+            nc.vector.scalar_tensor_tensor(
+                out=xns[b][:, cols], in0=ys[b][:, cols], scalar=rstd[:, b : b + 1], in1=shift[:, cols],
+                op0=ALU.mult, op1=ALU.add,
+            )
+            nc.sync.dma_start(out=out_1[b][:, cols], in_=xns[b][:, cols])
+
+        def spread(b):
+            diag = work.tile([P, P], F32, name="diag", bufs=4)
+            diags[b] = diag
+            nc.scalar.activation(out=diag[:], in_=ident[:], func=ACT.Copy, scale=rstd[:, b : b + 1])
+
+        def rescale(b):
+            n_banks[b] = mm_tile()
+            nc.tensor.matmul(out=n_banks[b][:], lhsT=diags[b][:], rhs=ys[b][:], start=True, stop=False)
+            nc.tensor.matmul(out=n_banks[b][:], lhsT=ident_b[:], rhs=shift[:], start=False, stop=True)
+
+        def finish(b, on_vector):
+            xn = work.tile([P, C], F32, name="xn", bufs=8)
+            either(on_vector)(out=xn[:], in_=n_banks[b][:])
+            nc.sync.dma_start(out=out_1[b], in_=xn[:])
+
         nc.gpsimd.tensor_copy(out=s2v[0:32, :], in_=s2b[:])
         warm_up(1)
         warm_up(1)
@@ -277,216 +321,250 @@ def tile_block_attention_guide_pb_kernel(
         warm_up(1)
         warm_up(1)
         warm_up(1)
-        warm_up(1)
-        g_widen(0, 0, False)
+        g_widen(1, False)
         w_transpose(0)
-        g_widen(0, 1, False)
+        g_widen(0, False)
         warm_up(1)
-        warm_up(1)
+        hot(0)
         w_copy(0, True)
+        hot(0)
         w_transpose(1)
         w_quant(0)
-        g_transpose(0, 1)
-        w_copy(1, True)
-        warm_up(1)
-        warm_up(1)
-        g_scale(0, 1)
+        g_widen(3, True)
         g_transpose(0, 0)
+        w_copy(1, False)
+        g_widen(2, True)
         warm_up(1)
+        warm_up(1)
+        a_scale(0, False)
+        g_scale(0, 0)
+        g_transpose(0, 1)
+        w_transpose(2)
+        a_scale(1, False)
         w_quant(1)
         warm_up(1)
-        g_scale(0, 0)
-        w_transpose(4)
-        w_transpose(6)
-        w_copy(4, False)
-        w_transpose(2)
-        g_quant(0)
-        w_copy(6, False)
+        g_scale(0, 1)
+        warm_up(1)
         w_transpose(3)
-        w_quant(4)
-        w_copy(2, True)
-        g_widen(1, 1, False)
-        h_matmul(0, 0, 1)
-        w_quant(6)
-        h_matmul(0, 0, 0)
-        w_quant(2)
-        w_copy(3, True)
-        h_matmul(0, 1, 0)
-        g_widen(1, 0, True)
-        h_bias(0, 0, 0, False)
-        w_transpose(5)
-        w_quant(3)
-        h_bias(0, 1, 0, False)
-        w_transpose(7)
-        h_bias(0, 0, 1, True)
-        w_copy(5, False)
-        h_matmul(0, 1, 1)
-        a_scale(0, True)
-        h_matmul(0, 3, 0)
-        w_copy(7, False)
-        h_matmul(0, 3, 1, 2)
-        w_quant(5)
-        h_bias(0, 1, 1, False)
-        g_transpose(1, 1)
+        w_copy(2, False)
         a_quant(0)
-        w_quant(7)
-        h_bias(0, 3, 0, False)
-        h_matmul(0, 1, 3)
-        a_scale(1, True)
-        h_bias(0, 3, 1, False)
-        h_matmul(0, 2, 0)
-        g_transpose(1, 0)
-        g_scale(1, 1)
-        h_bias(0, 1, 3, False)
-        h_matmul(0, 2, 1)
-        h_bias(0, 2, 0, False)
-        h_matmul(0, 0, 3)
+        w_transpose(4)
+        g_quant(0)
+        w_transpose(5)
+        w_quant(2)
+        w_copy(4, False)
+        w_copy(3, True)
+        h_matmul(0, 0, 1)
+        h_matmul(0, 0, 0)
+        w_copy(5, False)
         a_quant(1)
-        h_matmul(0, 1, 2, 2)
-        a_scale(2, False)
-        h_bias(0, 2, 1, True)
-        h_transpose(0, 0)
-        h_transpose(1, 0)
-        g_scale(1, 0)
-        h_matmul(0, 0, 2)
-        h_bias(0, 0, 3, False)
-        h_matmul(0, 2, 2)
-        h_copy(0, 0, True)
-        h_matmul(0, 2, 3)
-        h_bias(0, 1, 2, False)
-        h_matmul(0, 3, 3)
-        a_quant(2)
-        h_bias(0, 0, 2, False)
-        h_transpose(0, 1)
-        h_transpose(1, 1)
-        g_quant(1)
-        h_bias(0, 3, 3, False)
-        h_matmul(0, 3, 2, 2)
-        h_bias(0, 2, 3, True)
-        h_bias(0, 2, 2, False)
-        h_copy(0, 1, True)
-        h_matmul(1, 0, 0)
-        h_copy(1, 1, False)
-        h_matmul(1, 1, 1, 2)
-        h_copy(1, 0, True)
-        h_bias(0, 3, 2, False)
-        h_matmul(1, 0, 1)
-        h_quant(0, 0)
-        h_matmul(1, 2, 0)
-        h_bias(1, 0, 0, False)
-        h_transpose(0, 3)
-        h_transpose(1, 3)
-        h_quant(1, 0)
-        h_bias(1, 1, 1, False)
-        h_matmul(1, 1, 2)
-        h_bias(1, 2, 0, True)
-        h_bias(1, 0, 1, False)
-        h_matmul(1, 2, 1)
-        h_copy(0, 3, True)
-        h_matmul(1, 3, 1, 2)
-        h_bias(1, 1, 2, False)
-        h_matmul(1, 3, 0)
+        h_matmul(0, 1, 0)
+        w_quant(4)
+        h_matmul(0, 1, 1)
+        h_bias(0, 0, 1, False)
+        w_quant(3)
+        w_transpose(6)
+        h_bias(0, 0, 0, False)
+        h_bias(0, 1, 1, True)
+        h_matmul(0, 3, 1)
+        h_bias(0, 1, 0, False)
+        a_scale(2, True)
+        h_matmul(0, 2, 1)
+        h_matmul(0, 2, 0)
+        w_copy(6, False)
+        h_matmul(0, 3, 0)
         a_scale(3, True)
-        h_transpose(0, 2)
-        h_transpose(1, 2)
-        h_bias(1, 2, 1, False)
-        h_copy(1, 3, True)
-        h_bias(1, 3, 0, False)
-        h_matmul(1, 0, 2)
-        a_quant(3)
-        h_matmul(1, 1, 0)
-        h_bias(1, 3, 1, False)
-        h_copy(0, 2, True)
-        h_matmul(1, 3, 3, 2)
-        h_copy(1, 2, False)
-        h_bias(1, 1, 0, True)
-        h_matmul(1, 1, 3)
-        h_transpose(2, 1)
-        h_transpose(3, 1)
-        h_bias(1, 0, 2, False)
-        h_quant(0, 1)
-        h_bias(1, 1, 3, False)
+        h_matmul(0, 0, 3)
+        h_bias(0, 3, 1, False)
+        g_transpose(1, 0)
+        w_quant(6)
+        h_bias(0, 2, 0, False)
+        w_quant(5)
+        w_transpose(7)
+        h_bias(0, 2, 1, True)
+        h_bias(0, 3, 0, False)
+        h_matmul(0, 0, 2)
+        a_quant(2)
+        h_matmul(0, 2, 2)
+        w_copy(7, False)
+        g_scale(1, 0)
+        h_matmul(0, 1, 2)
+        h_matmul(0, 1, 3)
+        h_bias(0, 0, 3, False)
+        h_transpose(1, 1)
+        h_bias(0, 2, 2, False)
+        h_bias(0, 1, 2, True)
+        h_transpose(1, 0)
+        h_transpose(0, 0)
+        h_bias(0, 0, 2, False)
+        w_quant(7)
+        h_matmul(0, 2, 3)
+        h_copy(1, 1, True)
+        h_bias(0, 1, 3, False)
+        h_matmul(0, 3, 2)
+        h_matmul(0, 3, 3)
+        h_copy(1, 0, True)
+        h_copy(0, 0, False)
+        g_transpose(2, 0)
+        g_quant(1)
+        h_bias(0, 2, 3, False)
+        h_bias(0, 3, 2, True)
+        h_transpose(0, 1)
+        h_matmul(1, 3, 2, 2)
+        h_bias(0, 3, 3, False)
+        g_scale(2, 0)
         h_matmul(1, 0, 3)
-        h_quant(1, 1)
-        o_matmul(0)
-        h_copy(3, 1, False)
-        o_matmul(1)
-        h_bias(1, 3, 3, True)
-        h_copy(2, 1, False)
-        residual(0)
-        o_matmul(2)
+        h_matmul(1, 1, 1)
+        h_matmul(1, 3, 1)
+        h_copy(0, 1, False)
+        h_matmul(1, 0, 1)
+        h_transpose(0, 2)
+        h_bias(1, 1, 1, False)
+        h_bias(1, 3, 2, True)
+        h_transpose(0, 3)
+        h_bias(1, 0, 1, False)
+        g_quant(2)
+        h_transpose(1, 3)
         h_bias(1, 0, 3, False)
+        h_copy(0, 2, True)
+        h_matmul(1, 2, 1)
+        h_bias(1, 3, 1, False)
+        h_matmul(1, 0, 0)
+        h_matmul(2, 3, 1)
+        h_quant(0, 0)
+        h_copy(0, 3, False)
+        h_matmul(1, 1, 2, 2)
+        h_matmul(1, 2, 0)
+        h_transpose(1, 2)
+        h_bias(2, 3, 1, False)
+        h_bias(1, 2, 1, True)
+        h_bias(1, 0, 0, False)
+        h_quant(0, 1)
+        h_matmul(1, 1, 3)
+        h_bias(1, 1, 2, False)
+        h_matmul(1, 2, 3)
+        h_matmul(1, 3, 0, 2)
+        a_quant(3)
+        h_bias(1, 2, 0, False)
+        o_matmul(1)
+        h_copy(1, 2, False)
+        h_quant(1, 0)
+        o_matmul(0)
+        h_transpose(2, 1)
+        h_bias(1, 1, 3, False)
+        h_bias(1, 2, 3, True)
+        h_bias(1, 3, 0, False)
         residual(1)
-        o_matmul(3)
-        variance(0)
-        h_transpose(2, 0)
-        h_transpose(3, 0)
-        residual(2)
+        h_matmul(2, 2, 2)
+        h_copy(1, 3, False)
+        h_matmul(1, 2, 2)
+        h_matmul(1, 3, 3)
+        residual(0)
+        h_matmul(1, 0, 2, 2)
+        h_bias(2, 2, 2, False)
+        average(1)
+        h_bias(1, 3, 3, False)
+        h_quant(1, 1)
+        h_matmul(2, 0, 0)
+        h_matmul(2, 1, 2)
+        h_bias(1, 2, 2, False)
         average(0)
         variance(1)
-        h_matmul(1, 3, 2)
+        h_bias(1, 0, 2, True)
+        h_matmul(1, 1, 0)
+        h_matmul(2, 1, 0)
+        h_copy(2, 1, True)
+        o_matmul(3)
+        h_bias(2, 0, 0, False)
+        h_transpose(2, 3)
         centre(0)
-        h_matmul(1, 2, 2, 2)
+        h_bias(2, 1, 2, False)
+        h_transpose(2, 2)
+        h_bias(2, 1, 0, False)
+        h_matmul(2, 2, 0, 2)
+        residual(3)
+        deviation(1)
+        h_bias(1, 1, 0, False)
+        o_matmul(2)
+        variance(0)
+        h_copy(2, 3, True)
+        h_matmul(2, 3, 3)
+        h_matmul(2, 3, 2)
+        h_matmul(2, 1, 1, 2)
+        average(3)
+        h_copy(2, 2, False)
+        h_transpose(2, 0)
+        residual(2)
+        h_bias(2, 3, 3, False)
+        h_bias(2, 2, 0, True)
+        h_bias(2, 3, 2, False)
+        h_quant(2, 1)
+        h_matmul(2, 2, 1)
+        h_copy(2, 0, False)
+        h_matmul(2, 0, 3)
+        h_matmul(2, 2, 3, 2)
+        centre(1)
+        h_bias(2, 1, 1, False)
+        h_matmul(2, 1, 3)
         average(2)
+        h_bias(2, 2, 1, False)
+        h_matmul(2, 0, 2)
+        h_quant(2, 0)
+        h_bias(2, 0, 3, False)
+        h_matmul(2, 0, 1)
+        h_bias(2, 2, 3, False)
+        h_matmul(2, 3, 0, 2)
+        normalise(1)
         deviation(0)
         variance(2)
-        h_copy(2, 0, True)
-        h_matmul(1, 2, 3)
-        deviation(1)
-        h_bias(1, 2, 2, True)
-        h_bias(1, 3, 2, False)
-        normalise(0)
-        h_bias(1, 2, 3, False)
-        h_transpose(2, 2)
-        h_transpose(3, 2)
-        h_quant(2, 0)
-        deviation(2)
-        average(1)
-        h_copy(3, 0, False)
-        centre(1)
-        h_copy(2, 2, False)
-        h_quant(3, 0)
-        h_copy(3, 2, False)
-        h_transpose(2, 3)
-        h_transpose(3, 3)
-        normalise(1)
-        residual(3)
-        h_copy(3, 3, False)
-        centre(2)
-        h_copy(2, 3, False)
-        h_quant(3, 1)
-        variance(3)
-        h_quant(2, 1)
-        average(3)
-        o_matmul(6)
-        deviation(3)
-        centre(3)
-        o_matmul(4)
-        normalise(2)
-        normalise(3)
-        o_matmul(7)
-        residual(6)
         o_matmul(5)
+        centre(2)
+        h_bias(2, 3, 0, False)
+        normalise(0)
+        h_bias(2, 1, 3, False)
+        h_transpose(3, 0)
+        h_bias(2, 0, 2, False)
+        centre(3)
+        h_bias(2, 0, 1, False)
+        o_matmul(4)
+        variance(3)
+        residual(5)
+        h_transpose(3, 1)
+        deviation(2)
+        h_copy(3, 0, False)
+        h_transpose(3, 3)
         residual(4)
+        deviation(3)
+        h_copy(3, 1, False)
+        h_transpose(3, 2)
+        normalise(2)
+        h_copy(3, 3, False)
+        normalise(3)
+        h_copy(3, 2, False)
+        h_quant(3, 0)
+        average(5)
+        average(4)
+        variance(5)
+        h_quant(3, 1)
+        variance(4)
+        centre(5)
+        o_matmul(7)
+        centre(4)
+        deviation(4)
+        deviation(5)
+        o_matmul(6)
+        normalise(5)
+        residual(7)
+        residual(6)
+        average(7)
+        variance(7)
+        centre(7)
+        deviation(7)
         average(6)
         variance(6)
-        centre(6)
-        variance(4)
-        residual(5)
-        deviation(6)
-        average(4)
-        deviation(4)
-        residual(7)
-        average(5)
-        variance(5)
-        centre(4)
-        variance(7)
-        normalise(6)
-        deviation(5)
-        average(7)
-        deviation(7)
         normalise(4)
-        centre(5)
-        centre(7)
-        normalise(5)
         normalise(7)
+        deviation(6)
+        centre(6)
+        normalise_part(6, 1)
+        normalise_part(6, 0)

from contextlib import ExitStack

import concourse.mybir as mybir
from concourse.masks import make_identity

F32 = mybir.dt.float32
BF16 = mybir.dt.bfloat16
U32 = mybir.dt.uint32
U8 = mybir.dt.uint8
FP8 = mybir.dt.float8_e4m3fn
FP8X4 = mybir.dt.float8_e4m3fn_x4
ALU = mybir.AluOpType
ACT = mybir.ActivationFunctionType

B, J, C, K = 8, 128, 512, 4
P = 128
PAIRS = B // 2
NCC = C // P
EPS = 1e-5

FLOPS = 2 * B * J * C * K * C + 2 * B * K * J * J * C

TP_BANKS = 3
GROUPS = ((0, 1), (2,), (3,))


def tile_block_attention_guide_pb_kernel(
    tc, g1_bytes, g1_scale, res1, adj, spatial_adj, conv2_w, conv2_b, s2, norm2_g, norm2_b, out_0, out_1
):
    nc = tc.nc
    with ExitStack() as ctx:
        keep = ctx.enter_context(tc.tile_pool(name="keep", bufs=1))
        work = ctx.enter_context(tc.tile_pool(name="work", bufs=3))
        psum = ctx.enter_context(tc.psum_pool(name="psum", bufs=1))
        ctx.enter_context(tc.manual_schedule())

        def keep_tile(name, shape, dt):
            return keep.tile(shape, dt, name=name, align_bytes=64)

        sizes = [len(pairs) for pairs in GROUPS]
        gb = [keep_tile("gb%d" % p, [P, 2, C], U8) for p in range(PAIRS)]
        gw = [keep_tile("gw%d" % p, [P, 2, C], BF16) for p in range(PAIRS)]
        gs = [keep_tile("gs%d" % g, [P, 2 * J * n, 4], BF16) for g, n in enumerate(sizes)]
        gc = [keep_tile("gc%d" % g, [P, 2 * J * n], U32) for g, n in enumerate(sizes)]
        gsc = [keep_tile("gsc%d" % g, [P, 2 * J * n], U8) for g, n in enumerate(sizes)]
        wr = [keep_tile("wr%d" % j, [P, 2, C], BF16) for j in range(8)]
        wi = [keep_tile("wi%d" % j, [P, 2 * P, 4], BF16) for j in range(8)]
        wc = [keep_tile("wc%d" % j, [P, 2 * P], U32) for j in range(8)]
        wsc = [keep_tile("wsc%d" % j, [P, 2 * P], U8) for j in range(8)]
        hh = [[keep_tile("hh%d_%d" % (g, cc), [P, 4 * n, K, J // 2], BF16) for cc in range(NCC)] for g, n in enumerate(sizes)]
        hq = [[keep_tile("hq%d_%d" % (p, f), [P, 2, C // 2, 4], BF16) for f in range(2)] for p in range(PAIRS)]
        hc = [[keep_tile("hc%d_%d" % (p, f), [P, C], U32) for f in range(2)] for p in range(PAIRS)]
        hsc = [[keep_tile("hsc%d_%d" % (p, f), [P, C], U8) for f in range(2)] for p in range(PAIRS)]
        a_raw = [keep_tile("a_raw%d" % p, [P, 2, 4, J], BF16) for p in range(PAIRS)]
        a_bf = [keep_tile("a_bf%d" % p, [P, 2, J, 4], BF16) for p in range(PAIRS)]
        ac = [keep_tile("ac%d" % p, [P, 2 * J], U32) for p in range(PAIRS)]
        asc = [keep_tile("asc%d" % p, [P, 2 * J], U8) for p in range(PAIRS)]
        res = [keep_tile("res%d" % p, [P, 2, C], BF16) for p in range(PAIRS)]
        ident = keep_tile("ident", [P, P], F32)
        perm = keep_tile("perm", [P, P], F32)
        ident_b = keep_tile("ident_b", [P, P], BF16)
        bias = keep_tile("bias", [P, K, NCC], BF16)
        gsv = keep_tile("gsv", [P, 4], F32)
        s2b = keep_tile("s2b", [32, 1], BF16)
        s2v = keep_tile("s2v", [P, 1], F32)
        gain = keep_tile("gain", [P, C], BF16)
        shift = keep_tile("shift", [P, C], BF16)
        sums = keep_tile("sums", [P, B], F32)
        mean = keep_tile("mean", [P, B], F32)
        ssq = keep_tile("ssq", [P, B], F32)
        rstd = keep_tile("rstd", [P, B], F32)
        eps = keep_tile("eps", [P, 1], F32)
        warm = keep_tile("warm", [P, 1], F32)
        zeros = keep_tile("zeros", [P, 512], BF16)

        def tp_tile():
            return psum.tile([P, 512], F32, name="tp", bufs=TP_BANKS)

        def mm_tile():
            return psum.tile([P, 512], F32, name="mm", bufs=8 - TP_BANKS)

        g_src = g1_bytes.rearrange("(p bb) (v e) c -> p (bb v) (e c)", bb=2, e=2)
        w_src = conv2_w.rearrange("(k m f cc) c -> f k m cc c", k=K, m=P, f=2)
        r_src = res1.rearrange("b j c -> j b c")

        def load_g(p):
            nc.sync.dma_start(out=gb[p][:].rearrange("p e c -> p (e c)"), in_=g_src[p])

        def load_w(j):
            nc.sync.dma_start(out=wr[j][:], in_=w_src[j // 4][j % 4])

        adj_src = adj.rearrange("b o (q t) w -> q b (o t w)", t=4)
        spatial_src = spatial_adj.rearrange("k (q t) w -> (k q) (t w)", t=4).unsqueeze(1).to_broadcast([96, 2, 4 * J])

        def load_a(p):
            nc.sync.dma_start(out=a_raw[p][0:32, :, :, :].rearrange("p b t w -> p b (t w)"), in_=adj_src[:, 2 * p : 2 * p + 2, :])
            nc.sync.dma_start(out=a_raw[p][32:P, :, :, :].rearrange("p b t w -> p b (t w)"), in_=spatial_src)

        def load_r(p):
            nc.sync.dma_start(out=res[p][:], in_=r_src[:, 2 * p : 2 * p + 2, :])

        for p in GROUPS[0]:
            load_g(p)
        nc.vector.memset(zeros[:].bitcast(U32), 0)
        nc.vector.memset(warm[:], 0.0)
        nc.scalar.dma_start(out=gsv[:], in_=g1_scale.rearrange("a b (p t) -> p (a b t)", t=4))
        nc.scalar.dma_start(out=s2b[:], in_=s2.partition_broadcast(32))
        nc.scalar.dma_start(out=bias[:], in_=conv2_b.rearrange("(k m cc) -> m k cc", k=K, cc=NCC))
        nc.vector.tensor_scalar(out=eps[:], in0=warm[:], scalar1=EPS, scalar2=None, op0=ALU.add)
        nc.scalar.activation(out=warm[:], in_=eps[:], func=ACT.Abs_reciprocal_sqrt)
        make_identity(nc, ident[:])
        nc.gpsimd.memset(s2v[:], 1.0)
        load_w(0)
        load_w(1)
        for p in range(len(GROUPS[0]), PAIRS):
            load_g(p)
        load_a(0)
        load_w(2)
        load_a(1)
        for j in range(3, 8):
            load_w(j)
        load_a(2)
        load_a(3)
        load_r(0)
        nc.sync.dma_start(out=gain[:], in_=norm2_g.partition_broadcast(P))
        nc.sync.dma_start(out=shift[:], in_=norm2_b.partition_broadcast(P))
        for p in range(1, PAIRS):
            load_r(p)

        nc.vector.tensor_copy(
            out=perm[:].rearrange("p (x u q) -> p x u q", x=2, u=2),
            in_=ident[:].rearrange("p (x q u) -> p x u q", x=2, u=2),
        )

        nc.vector.tensor_copy(out=ident_b[:], in_=ident[:])

        g_banks, w_banks, h_banks, t_banks, o_banks, n_banks, x2s, ys, diags, xns = {}, {}, {}, {}, {}, {}, {}, {}, {}, {}

        def either(on_vector):
            return nc.vector.tensor_copy if on_vector else nc.scalar.copy

        def warm_up(n):
            bank = mm_tile()
            for r in range(n):
                nc.tensor.matmul(out=bank[:], lhsT=zeros[:, 0:P], rhs=zeros[:], start=True, stop=True)

        def hot(j):
            bank = mm_tile()
            nc.tensor.matmul(out=bank[:], lhsT=zeros[:, 0:P], rhs=wr[j][:, 0, :], start=True, stop=True)

        def g_widen(p, on_vector):
            either(on_vector)(out=gw[p][:], in_=gb[p][:].bitcast(FP8))

        def g_transpose(g, s):
            bank = tp_tile()
            g_banks[(g, s)] = bank
            parts = [(p, s) for p in GROUPS[g]] if sizes[g] == 2 else [(GROUPS[g][0], e) for e in range(2)]
            for y, (p, e) in enumerate(parts):
                words = gw[p][:, e, :].bitcast(F32)
                for u in range(2):
                    o = 256 * u + 128 * y
                    nc.tensor.transpose(bank[:, o : o + 128], words[:, u::2], perm[:])

        def g_scale(g, s):
            nc.vector.tensor_tensor(
                out=gs[g][:, 256 * s : 256 * s + 256, :].rearrange("p r (u e) -> p r u e", u=2),
                in0=g_banks[(g, s)][:].bitcast(BF16).rearrange("p (u r e) -> p r u e", u=2, e=2),
                in1=gsv[:].rearrange("p (u e) -> p u e", u=2).unsqueeze(1).to_broadcast([P, 256, 2, 2]),
                op=ALU.mult,
            )

        def g_quant(g):
            nc.vector.quantize_mx(out=gc[g][:].bitcast(FP8X4), scales=gsc[g][:], in_=gs[g][:].rearrange("p r t -> p (r t)"))

        def w_transpose(j):
            bank = tp_tile()
            w_banks[j] = bank
            for kk in range(2):
                words = wr[j][:, kk, :].bitcast(F32)
                for u in range(2):
                    o = 256 * u + 128 * kk
                    nc.tensor.transpose(bank[:, o : o + 128], words[:, u::2], ident[:])

        def w_copy(j, on_vector):
            either(on_vector)(
                out=wi[j][:].rearrange("p m t -> p (m t)").bitcast(F32).rearrange("p (m u) -> p m u", u=2),
                in_=w_banks[j][:].rearrange("p (u m) -> p m u", u=2),
            )

        def w_quant(j):
            nc.vector.quantize_mx(out=wc[j][:].bitcast(FP8X4), scales=wsc[j][:], in_=wi[j][:].rearrange("p m t -> p (m t)"))

        def a_scale(p, on_vector):
            src = a_raw[p][:].rearrange("p b t w -> p b w t")
            if on_vector:
                nc.vector.tensor_scalar(out=a_bf[p][:], in0=src, scalar1=s2v[:, 0:1], scalar2=None, op0=ALU.mult)
            else:
                nc.scalar.activation(out=a_bf[p][:], in_=src, func=ACT.Copy, scale=s2v[:, 0:1])

        def a_quant(p):
            nc.vector.quantize_mx(out=ac[p][:].bitcast(FP8X4), scales=asc[p][:], in_=a_bf[p][:].rearrange("p b w t -> p (b w t)"))

        def h_matmul(h, k, cc, times=1):
            j, cols, n = 4 * (cc // 2) + k, slice(P * (cc % 2), P * (cc % 2) + P), 2 * J * sizes[h]
            bank = mm_tile()
            h_banks[(h, k, cc)] = bank
            for r in range(times):
                nc.tensor.matmul_mx(
                    out=bank[:, 0:n], lhsT=wc[j][:, cols].bitcast(FP8X4), lhsT_scale=wsc[j][:, cols],
                    rhs=gc[h][:].bitcast(FP8X4), rhs_scale=gsc[h][:], start=True, stop=True,
                )

        def h_bias(h, k, cc, on_vector):
            out = hh[h][cc][:, :, k, :].rearrange("p x (q e) -> p x q e", e=2)
            src = h_banks[(h, k, cc)][:, 0 : 2 * J * sizes[h]].rearrange("p (e x q) -> p x q e", e=2, q=32)
            col = bias[:, k, cc : cc + 1]
            if on_vector:
                nc.vector.tensor_scalar(out=out, in0=src, scalar1=col, scalar2=None, op0=ALU.add)
            else:
                nc.scalar.activation(out=out, in_=src, func=ACT.Identity, bias=col)

        def h_transpose(p, cc):
            bank = tp_tile()
            t_banks[(p, cc)] = bank
            g = [p in pairs for pairs in GROUPS].index(True)
            for x in range(4):
                words = hh[g][cc][:, 4 * GROUPS[g].index(p) + x, :, :].rearrange("p k v -> p (k v)").bitcast(F32)
                nc.tensor.transpose(bank[:, 128 * x : 128 * x + 128], words, ident[:])

        def h_copy(p, cc, on_vector):
            c0 = P * (cc % 2)
            dst = hq[p][cc // 2][:, :, c0 : c0 + P, :].rearrange("p b c t -> p b (c t)").bitcast(F32)
            either(on_vector)(
                out=dst.rearrange("p b (c u) -> p b c u", u=2),
                in_=t_banks[(p, cc)][:].rearrange("p (b u c) -> p b c u", b=2, u=2),
            )

        def h_quant(p, f):
            nc.vector.quantize_mx(
                out=hc[p][f][:].bitcast(FP8X4), scales=hsc[p][f][:], in_=hq[p][f][:].rearrange("p b c t -> p (b c t)")
            )

        def o_matmul(b):
            p, cols, half = b // 2, slice(J * (b % 2), J * (b % 2) + J), slice(256 * (b % 2), 256 * (b % 2) + 256)
            o_banks[b] = mm_tile()
            for f in range(2):
                nc.tensor.matmul_mx(
                    out=o_banks[b][:, 256 * f : 256 * f + 256],
                    lhsT=ac[p][:, cols].bitcast(FP8X4), lhsT_scale=asc[p][:, cols],
                    rhs=hc[p][f][:, half].bitcast(FP8X4), rhs_scale=hsc[p][f][:, half], start=True, stop=True,
                )

        def residual(b):
            x2 = work.tile([P, C], F32, name="x2", bufs=8)
            x2s[b] = x2
            nc.vector.scalar_tensor_tensor(
                out=x2[:].rearrange("p (m c) -> p m c", c=NCC), in0=o_banks[b][:].rearrange("p (c m) -> p m c", c=NCC),
                scalar=1.0, in1=res[b // 2][:, b % 2, :].rearrange("p (m c) -> p m c", c=NCC),
                op0=ALU.mult, op1=ALU.add, accum_out=sums[:, b : b + 1],
            )
            nc.sync.dma_start(out=out_0[b], in_=x2[:])

        def average(b):
            nc.scalar.activation(out=mean[:, b : b + 1], in_=sums[:, b : b + 1], func=ACT.Copy, scale=1.0 / C)

        def variance(b):
            junk = work.tile([P, C], BF16, name="junk", bufs=2)
            nc.scalar.activation(
                out=junk[:], in_=x2s[b][:], func=ACT.Square, scale=-float(C), bias=sums[:, b : b + 1],
                accum_out=ssq[:, b : b + 1],
            )

        def deviation(b):
            nc.scalar.activation(
                out=rstd[:, b : b + 1], in_=ssq[:, b : b + 1], func=ACT.Abs_reciprocal_sqrt, scale=1.0 / C**3, bias=eps[:, 0:1]
            )

        def centre(b):
            y = work.tile([P, C], F32, name="y", bufs=8)
            ys[b] = y
            nc.vector.scalar_tensor_tensor(
                out=y[:], in0=x2s[b][:], scalar=mean[:, b : b + 1], in1=gain[:], op0=ALU.subtract, op1=ALU.mult
            )

        def normalise(b):
            xn = work.tile([P, C], F32, name="xn", bufs=8)
            nc.vector.scalar_tensor_tensor(
                out=xn[:], in0=ys[b][:], scalar=rstd[:, b : b + 1], in1=shift[:], op0=ALU.mult, op1=ALU.add
            )
            nc.sync.dma_start(out=out_1[b], in_=xn[:])

        def normalise_part(b, s):
            if b not in xns:
                xns[b] = work.tile([P, C], F32, name="xn", bufs=8)
            cols = slice(256 * s, 256 * s + 256)
            nc.vector.scalar_tensor_tensor(
                out=xns[b][:, cols], in0=ys[b][:, cols], scalar=rstd[:, b : b + 1], in1=shift[:, cols],
                op0=ALU.mult, op1=ALU.add,
            )
            nc.sync.dma_start(out=out_1[b][:, cols], in_=xns[b][:, cols])

        def spread(b):
            diag = work.tile([P, P], F32, name="diag", bufs=4)
            diags[b] = diag
            nc.scalar.activation(out=diag[:], in_=ident[:], func=ACT.Copy, scale=rstd[:, b : b + 1])

        def rescale(b):
            n_banks[b] = mm_tile()
            nc.tensor.matmul(out=n_banks[b][:], lhsT=diags[b][:], rhs=ys[b][:], start=True, stop=False)
            nc.tensor.matmul(out=n_banks[b][:], lhsT=ident_b[:], rhs=shift[:], start=False, stop=True)

        def finish(b, on_vector):
            xn = work.tile([P, C], F32, name="xn", bufs=8)
            either(on_vector)(out=xn[:], in_=n_banks[b][:])
            nc.sync.dma_start(out=out_1[b], in_=xn[:])

        nc.gpsimd.tensor_copy(out=s2v[0:32, :], in_=s2b[:])
        warm_up(1)
        warm_up(1)
        warm_up(1)
        warm_up(1)
        warm_up(1)
        warm_up(1)
        g_widen(1, False)
        w_transpose(0)
        g_widen(0, False)
        warm_up(1)
        hot(0)
        w_copy(0, True)
        hot(0)
        w_transpose(1)
        w_quant(0)
        g_widen(3, True)
        g_transpose(0, 0)
        w_copy(1, False)
        g_widen(2, True)
        warm_up(1)
        warm_up(1)
        a_scale(0, False)
        g_scale(0, 0)
        g_transpose(0, 1)
        w_transpose(2)
        a_scale(1, False)
        w_quant(1)
        warm_up(1)
        g_scale(0, 1)
        warm_up(1)
        w_transpose(3)
        w_copy(2, False)
        a_quant(0)
        w_transpose(4)
        g_quant(0)
        w_transpose(5)
        w_quant(2)
        w_copy(4, False)
        w_copy(3, True)
        h_matmul(0, 0, 1)
        h_matmul(0, 0, 0)
        w_copy(5, False)
        a_quant(1)
        h_matmul(0, 1, 0)
        w_quant(4)
        h_matmul(0, 1, 1)
        h_bias(0, 0, 1, False)
        w_quant(3)
        w_transpose(6)
        h_bias(0, 0, 0, False)
        h_bias(0, 1, 1, True)
        h_matmul(0, 3, 1)
        h_bias(0, 1, 0, False)
        a_scale(2, True)
        h_matmul(0, 2, 1)
        h_matmul(0, 2, 0)
        w_copy(6, False)
        h_matmul(0, 3, 0)
        a_scale(3, True)
        h_matmul(0, 0, 3)
        h_bias(0, 3, 1, False)
        g_transpose(1, 0)
        w_quant(6)
        h_bias(0, 2, 0, False)
        w_quant(5)
        w_transpose(7)
        h_bias(0, 2, 1, True)
        h_bias(0, 3, 0, False)
        h_matmul(0, 0, 2)
        a_quant(2)
        h_matmul(0, 2, 2)
        w_copy(7, False)
        g_scale(1, 0)
        h_matmul(0, 1, 2)
        h_matmul(0, 1, 3)
        h_bias(0, 0, 3, False)
        h_transpose(1, 1)
        h_bias(0, 2, 2, False)
        h_bias(0, 1, 2, True)
        h_transpose(1, 0)
        h_transpose(0, 0)
        h_bias(0, 0, 2, False)
        w_quant(7)
        h_matmul(0, 2, 3)
        h_copy(1, 1, True)
        h_bias(0, 1, 3, False)
        h_matmul(0, 3, 2)
        h_matmul(0, 3, 3)
        h_copy(1, 0, True)
        h_copy(0, 0, False)
        g_transpose(2, 0)
        g_quant(1)
        h_bias(0, 2, 3, False)
        h_bias(0, 3, 2, True)
        h_transpose(0, 1)
        h_matmul(1, 3, 2, 2)
        h_bias(0, 3, 3, False)
        g_scale(2, 0)
        h_matmul(1, 0, 3)
        h_matmul(1, 1, 1)
        h_matmul(1, 3, 1)
        h_copy(0, 1, False)
        h_matmul(1, 0, 1)
        h_transpose(0, 2)
        h_bias(1, 1, 1, False)
        h_bias(1, 3, 2, True)
        h_transpose(0, 3)
        h_bias(1, 0, 1, False)
        g_quant(2)
        h_transpose(1, 3)
        h_bias(1, 0, 3, False)
        h_copy(0, 2, True)
        h_matmul(1, 2, 1)
        h_bias(1, 3, 1, False)
        h_matmul(1, 0, 0)
        h_matmul(2, 3, 1)
        h_quant(0, 0)
        h_copy(0, 3, False)
        h_matmul(1, 1, 2, 2)
        h_matmul(1, 2, 0)
        h_transpose(1, 2)
        h_bias(2, 3, 1, False)
        h_bias(1, 2, 1, True)
        h_bias(1, 0, 0, False)
        h_quant(0, 1)
        h_matmul(1, 1, 3)
        h_bias(1, 1, 2, False)
        h_matmul(1, 2, 3)
        h_matmul(1, 3, 0, 2)
        a_quant(3)
        h_bias(1, 2, 0, False)
        o_matmul(1)
        h_copy(1, 2, False)
        h_quant(1, 0)
        o_matmul(0)
        h_transpose(2, 1)
        h_bias(1, 1, 3, False)
        h_bias(1, 2, 3, True)
        h_bias(1, 3, 0, False)
        residual(1)
        h_matmul(2, 2, 2)
        h_copy(1, 3, False)
        h_matmul(1, 2, 2)
        h_matmul(1, 3, 3)
        residual(0)
        h_matmul(1, 0, 2, 2)
        h_bias(2, 2, 2, False)
        average(1)
        h_bias(1, 3, 3, False)
        h_quant(1, 1)
        h_matmul(2, 0, 0)
        h_matmul(2, 1, 2)
        h_bias(1, 2, 2, False)
        average(0)
        variance(1)
        h_bias(1, 0, 2, True)
        h_matmul(1, 1, 0)
        h_matmul(2, 1, 0)
        h_copy(2, 1, True)
        o_matmul(3)
        h_bias(2, 0, 0, False)
        h_transpose(2, 3)
        centre(0)
        h_bias(2, 1, 2, False)
        h_transpose(2, 2)
        h_bias(2, 1, 0, False)
        h_matmul(2, 2, 0, 2)
        residual(3)
        deviation(1)
        h_bias(1, 1, 0, False)
        o_matmul(2)
        variance(0)
        h_copy(2, 3, True)
        h_matmul(2, 3, 3)
        h_matmul(2, 3, 2)
        h_matmul(2, 1, 1, 2)
        average(3)
        h_copy(2, 2, False)
        h_transpose(2, 0)
        residual(2)
        h_bias(2, 3, 3, False)
        h_bias(2, 2, 0, True)
        h_bias(2, 3, 2, False)
        h_quant(2, 1)
        h_matmul(2, 2, 1)
        h_copy(2, 0, False)
        h_matmul(2, 0, 3)
        h_matmul(2, 2, 3, 2)
        centre(1)
        h_bias(2, 1, 1, False)
        h_matmul(2, 1, 3)
        average(2)
        h_bias(2, 2, 1, False)
        h_matmul(2, 0, 2)
        h_quant(2, 0)
        h_bias(2, 0, 3, False)
        h_matmul(2, 0, 1)
        h_bias(2, 2, 3, False)
        h_matmul(2, 3, 0, 2)
        normalise(1)
        deviation(0)
        variance(2)
        o_matmul(5)
        centre(2)
        h_bias(2, 3, 0, False)
        normalise(0)
        h_bias(2, 1, 3, False)
        h_transpose(3, 0)
        h_bias(2, 0, 2, False)
        centre(3)
        h_bias(2, 0, 1, False)
        o_matmul(4)
        variance(3)
        residual(5)
        h_transpose(3, 1)
        deviation(2)
        h_copy(3, 0, False)
        h_transpose(3, 3)
        residual(4)
        deviation(3)
        h_copy(3, 1, False)
        h_transpose(3, 2)
        normalise(2)
        h_copy(3, 3, False)
        normalise(3)
        h_copy(3, 2, False)
        h_quant(3, 0)
        average(5)
        average(4)
        variance(5)
        h_quant(3, 1)
        variance(4)
        centre(5)
        o_matmul(7)
        centre(4)
        deviation(4)
        deviation(5)
        o_matmul(6)
        normalise(5)
        residual(7)
        residual(6)
        average(7)
        variance(7)
        centre(7)
        deviation(7)
        average(6)
        variance(6)
        normalise(4)
        normalise(7)
        deviation(6)
        centre(6)
        normalise_part(6, 1)
        normalise_part(6, 0)
